import numpy as np
import ml_dtypes

BF16 = ml_dtypes.bfloat16


def bf(x):
    return np.asarray(x, np.float32).astype(BF16)


def f32(x):
    return np.asarray(x, np.float32)


def f64(x):
    return np.asarray(x).astype(np.float64)


def striped(idx):
    return np.tile(idx.reshape(-1, 16).T, (8, 1))


C, S, N, B, T, NH, NS, HN, PAIR = 512, 2048, 1024, 2, 512, 4, 256, 1024, 2
EPS = 1e-5
THETA = 2.0 ** 16


def ln(v, axis):
    m = v.mean(axis=axis, keepdims=True)
    d = v - m
    return d / np.sqrt((d * d).mean(axis=axis, keepdims=True) + EPS)


def rope_tables():
    q = np.repeat(np.arange(NS // PAIR) * PAIR, PAIR) / NS
    ang = (THETA ** (-q))[:, None] * np.arange(T)[None, :]
    sign = np.tile(np.array([-1.0, 1.0]), NS // PAIR)[:, None]
    return np.cos(ang), sign * np.sin(ang)


def setup_inputs():
    cs, sn = rope_tables()
    return {
        "table": f32(np.random.standard_normal((C, S))),
        "h_init": f32(0.5 * np.random.standard_normal((C, 1))),
        "l_init": f32(0.5 * np.random.standard_normal((C, 1))),
        "enc": bf(0.5 * np.random.standard_normal((C, HN)) / np.sqrt(C)),
        "enc_v": bf(np.random.standard_normal((C, HN)) / np.sqrt(C)),
        "dec": bf(2.0 * np.random.standard_normal((HN, C)) / np.sqrt(HN)),
        "cos_t": f32(cs),
        "sin_t": f32(sn),
        "offs": striped(np.random.permutation(np.tile(np.arange(S), 2))[:N]),
    }


def reference(table, h_init, l_init, enc, enc_v, dec, cos_t, sin_t, offs):
    idx = offs[:16].T.reshape(-1)
    tn = ln(f64(table), 0)
    u = tn[:, idx] + (f64(h_init) + f64(l_init))
    xi = ln(u, 0)
    xs = np.maximum(f64(enc).T @ xi, 0.0)
    sw = xs.reshape(HN // PAIR, PAIR, N)[:, ::-1, :].reshape(HN, N)
    qr = xs * np.tile(f64(cos_t), (NH, B)) + sw * np.tile(f64(sin_t), (NH, B))
    mask = np.tril(np.ones((T, T)), -1)
    ev = f64(enc_v)
    ys = np.zeros((HN, N))
    for b in range(B):
        cols = slice(b * T, (b + 1) * T)
        for h in range(NH):
            rows = slice(h * NS, (h + 1) * NS)
            qb = qr[rows, cols]
            a = (qb.T @ qb) * NS ** -0.5 * mask
            av = xi[:, cols] @ a.T
            ys[rows, cols] = np.maximum(ev[:, rows].T @ ln(av, 0), 0.0)
    y = ln(f64(dec).T @ (xs * ys), 0)
    return ln(f64(l_init) + y, 0)

@@ -1,0 +1,303 @@
+import concourse.mybir as mybir
+from concourse.masks import make_identity
+
+F32 = mybir.dt.float32
+BF16 = mybir.dt.bfloat16
+U16 = mybir.dt.uint16
+ALU = mybir.AluOpType
+ACT = mybir.ActivationFunctionType
+AX = mybir.AxisListType
+
+P = 128
+C, S, N, B, T, NH, NS, HN = 512, 2048, 1024, 2, 512, 4, 256, 1024
+CB = C // P
+KB = HN // P
+RB = T // P
+W = 512
+EPS = 1e-5
+
+FLOPS = 2 * (C * HN * N + B * NH * (NS + C) * (T * (T - 1) // 2) + C * HN * N + HN * C * N)
+
+
+def tile_bdhhrm_b_kernel(tc, table, h_init, l_init, enc, enc_v, dec, cos_t, sin_t, offs, out):
+    nc = tc.nc
+    with (
+        tc.tile_pool(name="held", bufs=1) as held,
+        tc.tile_pool(name="pair", bufs=2) as pair,
+        tc.tile_pool(name="ring", bufs=3) as ring,
+        tc.psum_pool(name="psum", bufs=8) as psum,
+    ):
+
+        def bank(shape=(P, W), dtype=F32):
+            return psum.tile(list(shape), dtype, name="bank", tag="bank")
+
+        offsets = held.tile([P, N // 16], U16, name="offsets")
+        nc.sync.dma_start(offsets[:], offs)
+
+        mean_w32 = held.tile([P, P], F32, name="mean_w32")
+        nc.vector.memset(mean_w32[:], 1.0 / C)
+        mean_w16 = held.tile([P, P], BF16, name="mean_w16")
+        nc.vector.memset(mean_w16[:], 1.0 / C)
+        eps_t = held.tile([P, 1], F32, name="eps_t")
+        nc.vector.memset(eps_t[:], EPS)
+        ident = held.tile([P, P], BF16, name="ident")
+        make_identity(nc, ident[:])
+        later = held.tile([P, P], F32, name="later")
+        nc.gpsimd.memset(later[:], 1.0)
+        nc.gpsimd.affine_select(
+            out=later[:], in_=later[:], pattern=[[1, P]], compare_op=ALU.is_gt, fill=0.0, base=0, channel_multiplier=-1
+        )
+
+        def column_rstd(squares):
+            q_ps = bank()
+            for a in range(CB):
+                nc.tensor.matmul(q_ps[:], lhsT=mean_w16[:], rhs=squares[:, a, :], start=(a == 0), stop=(a == CB - 1))
+            rstd = ring.tile([P, W], F32, name="rstd")
+            nc.scalar.activation(out=rstd[:], in_=q_ps[:], func=ACT.Abs_reciprocal_sqrt, bias=eps_t[:, 0:1])
+            return rstd
+
+        h_t = held.tile([P, CB], F32, name="h_t")
+        l_t = held.tile([P, CB], F32, name="l_t")
+        with nc.allow_non_contiguous_dma(reason="512 values, one to a partition and block"):
+            nc.scalar.dma_start(h_t[:], h_init.rearrange("(a p) o -> p (a o)", p=P))
+            nc.scalar.dma_start(l_t[:], l_init.rearrange("(a p) o -> p (a o)", p=P))
+
+        xi = [held.tile([P, N], BF16, name=f"xi{a}") for a in range(CB)]
+        xi_t = [held.tile([P, C], BF16, name=f"xi_t{j}") for j in range(N // P)]
+        enc_sb = held.tile([P, CB, HN], BF16, name="enc_sb")
+        ev_sb = held.tile([P, CB, HN], BF16, name="ev_sb")
+        dec_sb = held.tile([P, KB, C], BF16, name="dec_sb")
+        cos_q = held.tile([P, 2, T], BF16, name="cos_q")
+        sin_x = held.tile([P, 2, T], BF16, name="sin_x")
+
+        with tc.tile_pool(name="front", bufs=1) as front:
+            tn = [front.tile([P, S], F32, name=f"tn{a}") for a in range(CB)]
+            for s in range(S // W):
+                for a in range(CB):
+                    nc.sync.dma_start(tn[a][:, s * W : (s + 1) * W], table[a * P : (a + 1) * P, s * W : (s + 1) * W])
+            nc.sync.dma_start(enc_sb[:], enc.rearrange("(a p) k -> p a k", p=P))
+            cos_raw = front.tile([P, 2, T], F32, name="cos_raw")
+            sin_raw = front.tile([P, 2, T], F32, name="sin_raw")
+            nc.sync.dma_start(cos_raw[:], cos_t.rearrange("(p e) t -> p e t", e=2))
+            nc.sync.dma_start(sin_raw[:], sin_t.rearrange("(p e) t -> p e t", e=2))
+            nc.sync.dma_start(ev_sb[:], enc_v.rearrange("(a p) k -> p a k", p=P))
+            for h in range(NH):
+                nc.sync.dma_start(
+                    dec_sb[:, 2 * h : 2 * h + 2, :], dec[h * NS : (h + 1) * NS, :].rearrange("(p e) c -> p e c", e=2)
+                )
+
+            both = held.tile([P, 2 * CB], F32, name="both")
+            nc.vector.tensor_tensor(out=both[:, 0:CB], in0=h_t[:], in1=l_t[:], op=ALU.add)
+            nc.vector.tensor_copy(both[:, CB : 2 * CB], l_t[:])
+            part_ps = bank((P, 2 * CB))
+            nc.tensor.matmul(part_ps[:], lhsT=mean_w32[:], rhs=both[:], start=True, stop=True)
+            means = held.tile([P, 2], F32, name="means")
+            centred = held.tile([P, 2 * CB], F32, name="centred")
+            for v in range(2):
+                nc.vector.reduce_sum(out=means[:, v : v + 1], in_=part_ps[:, v * CB : (v + 1) * CB], axis=AX.X)
+                nc.vector.tensor_scalar(
+                    out=centred[:, v * CB : (v + 1) * CB],
+                    in0=both[:, v * CB : (v + 1) * CB],
+                    scalar1=means[:, v : v + 1],
+                    scalar2=None,
+                    op0=ALU.subtract,
+                )
+            z0_c = centred[:, 0:CB]
+            l_c = centred[:, CB : 2 * CB]
+            z0_wide = [front.tile([P, W], F32, name=f"z0_wide{a}") for a in range(CB)]
+            for a in range(CB):
+                nc.vector.tensor_copy(z0_wide[a][:], z0_c[:, a : a + 1].to_broadcast([P, W]))
+
+            def mean_of(s):
+                cols = slice(s * W, (s + 1) * W)
+                m_ps = bank()
+                for a in range(CB):
+                    nc.tensor.matmul(m_ps[:], lhsT=mean_w32[:], rhs=tn[a][:, cols], start=(a == 0), stop=(a == CB - 1))
+                return m_ps
+
+            def centre(s, m_ps):
+                cols = slice(s * W, (s + 1) * W)
+                sq = ring.tile([P, CB, W], BF16, name="sq")
+                for a in range(CB):
+                    nc.vector.tensor_tensor(out=tn[a][:, cols], in0=tn[a][:, cols], in1=m_ps[:], op=ALU.subtract)
+                    nc.scalar.activation(out=sq[:, a, :], in_=tn[a][:, cols], func=ACT.Square)
+                return column_rstd(sq)
+
+            def scale(s, rstd):
+                cols = slice(s * W, (s + 1) * W)
+                for a in range(CB):
+                    nc.vector.tensor_tensor(out=tn[a][:, cols], in0=tn[a][:, cols], in1=rstd[:], op=ALU.mult)
+
+            pieces = S // W
+            m_next = mean_of(0)
+            for s in range(pieces):
+                m_now = m_next
+                if s + 1 < pieces:
+                    m_next = mean_of(s + 1)
+                rstd_now = centre(s, m_now)
+                if s > 0:
+                    scale(s - 1, rstd_before)
+                rstd_before = rstd_now
+            scale(pieces - 1, rstd_before)
+
+            u_c = [front.tile([P, N], F32, name=f"u_c{a}") for a in range(CB)]
+            for b in range(B):
+                for a in range(CB):
+                    nc.vector.tensor_tensor(
+                        out=u_c[a][:, b * T : (b + 1) * T],
+                        in0=tn[a][:].indirect(offsets[:, b * (T // 16) : (b + 1) * (T // 16)]),
+                        in1=z0_wide[a][:],
+                        op=ALU.add,
+                    )
+            for b in range(B):
+                tok = slice(b * T, (b + 1) * T)
+                sq = ring.tile([P, CB, W], BF16, name="sq")
+                for a in range(CB):
+                    nc.scalar.activation(out=sq[:, a, :], in_=u_c[a][:, tok], func=ACT.Square)
+                rstd = column_rstd(sq)
+                for a in range(CB):
+                    nc.vector.tensor_tensor(out=xi[a][:, tok], in0=u_c[a][:, tok], in1=rstd[:], op=ALU.mult)
+
+            nc.gpsimd.tensor_scalar(out=cos_q[:], in0=cos_raw[:], scalar1=0.25, scalar2=None, op0=ALU.mult)
+            for e in range(2):
+                nc.gpsimd.tensor_scalar(
+                    out=sin_x[:, e, :], in0=sin_raw[:, 1 - e, :], scalar1=0.25, scalar2=None, op0=ALU.mult
+                )
+
+        xs = held.tile([P, KB, N], BF16, name="xs")
+        qr = held.tile([P, KB, N], BF16, name="qr")
+        gated = held.tile([P, KB, N], BF16, name="gated")
+
+        def rows_of(h, e):
+            return slice(h * NS + e, (h + 1) * NS, 2)
+
+        def codes(b):
+            tok = slice(b * T, (b + 1) * T)
+            for h in range(NH):
+                for e in range(2):
+                    x_ps = bank()
+                    for a in range(CB):
+                        nc.tensor.matmul(
+                            x_ps[:], lhsT=enc_sb[:, a, rows_of(h, e)], rhs=xi[a][:, tok], start=(a == 0), stop=(a == CB - 1)
+                        )
+                    nc.scalar.activation(out=xs[:, 2 * h + e, tok], in_=x_ps[:], func=ACT.Relu)
+                own = pair.tile([P, 2, T], BF16, name="own")
+                other = pair.tile([P, 2, T], BF16, name="other")
+                nc.vector.tensor_tensor(out=own[:], in0=xs[:, 2 * h : 2 * h + 2, tok], in1=cos_q[:], op=ALU.mult)
+                nc.vector.tensor_tensor(out=other[:], in0=xs[:, 2 * h : 2 * h + 2, tok], in1=sin_x[:], op=ALU.mult)
+                for e in range(2):
+                    nc.vector.tensor_tensor(out=qr[:, 2 * h + e, tok], in0=own[:, e, :], in1=other[:, 1 - e, :], op=ALU.add)
+
+        codes(0)
+
+        for j in range(N // P):
+            t_ps = bank((P, C), BF16)
+            for a in range(CB):
+                nc.tensor.transpose(t_ps[:, a * P : (a + 1) * P], xi[a][:, j * P : (j + 1) * P], ident[:])
+            nc.scalar.copy(out=xi_t[j][:], in_=t_ps[:])
+
+        dec_c = held.tile([P, KB, C], BF16, name="dec_c")
+        neg_mean = held.tile([P, KB], F32, name="neg_mean")
+        for k in range(KB):
+            unused = pair.tile([P, C], BF16, name="unused")
+            nc.scalar.activation(
+                out=unused[:], in_=dec_sb[:, k, :], func=ACT.Copy, scale=-1.0 / C, accum_out=neg_mean[:, k : k + 1]
+            )
+            nc.gpsimd.tensor_scalar(
+                out=dec_c[:, k, :], in0=dec_sb[:, k, :], scalar1=neg_mean[:, k : k + 1], scalar2=None, op0=ALU.add
+            )
+
+        codes(1)
+
+        with tc.tile_pool(name="back", bufs=2) as back:
+            def scores(b, h):
+                a_t = back.tile([P, RB, T], BF16, name="a_t")
+                for i in range(RB):
+                    lo = i * P
+                    s_ps = bank()
+                    for e in range(2):
+                        nc.tensor.matmul(
+                            s_ps[:, lo:T],
+                            lhsT=qr[:, 2 * h + e, b * T + lo : b * T + lo + P],
+                            rhs=qr[:, 2 * h + e, b * T + lo : (b + 1) * T],
+                            start=(e == 0),
+                            stop=(e == 1),
+                        )
+                    nc.vector.tensor_tensor(out=a_t[:, i, lo : lo + P], in0=s_ps[:, lo : lo + P], in1=later[:], op=ALU.mult)
+                    if lo + P < T:
+                        nc.scalar.copy(out=a_t[:, i, lo + P : T], in_=s_ps[:, lo + P : T])
+                return a_t
+
+            def values(b, a_t):
+                av = back.tile([P, CB, T], BF16, name="av")
+                sq = ring.tile([P, CB, W], BF16, name="sq")
+                for a in range(CB):
+                    av_ps = bank()
+                    for i in range(RB):
+                        nc.tensor.matmul(
+                            av_ps[:, i * P : T],
+                            lhsT=xi_t[b * RB + i][:, a * P : (a + 1) * P],
+                            rhs=a_t[:, i, i * P : T],
+                            start=(i == 0),
+                            stop=(i == RB - 1),
+                        )
+                    nc.scalar.activation(out=sq[:, a, :], in_=av_ps[:], func=ACT.Square)
+                    nc.vector.tensor_copy(av[:, a, :], av_ps[:])
+                return av, sq
+
+            def gate(b, h, av, sq):
+                tok = slice(b * T, (b + 1) * T)
+                rstd = column_rstd(sq)
+                for e in range(2):
+                    v_ps = bank()
+                    for a in range(CB):
+                        nc.tensor.matmul(
+                            v_ps[:], lhsT=ev_sb[:, a, rows_of(h, e)], rhs=av[:, a, :], start=(a == 0), stop=(a == CB - 1)
+                        )
+                    prod = pair.tile([P, T], F32, name="prod")
+                    nc.vector.scalar_tensor_tensor(
+                        out=prod[:], in0=v_ps[:], scalar=0.0, in1=xs[:, 2 * h + e, tok], op0=ALU.max, op1=ALU.mult
+                    )
+                    nc.gpsimd.tensor_tensor(out=gated[:, 2 * h + e, tok], in0=prod[:], in1=rstd[:], op=ALU.mult)
+
+            def block_output(b):
+                tok = slice(b * T, (b + 1) * T)
+                w_ps = [bank() for a in range(CB)]
+                sq = ring.tile([P, CB, W], BF16, name="sq")
+                for a in range(CB):
+                    for k in range(KB):
+                        nc.tensor.matmul(
+                            w_ps[a][:],
+                            lhsT=dec_c[:, k, a * P : (a + 1) * P],
+                            rhs=gated[:, k, tok],
+                            start=(k == 0),
+                            stop=(k == KB - 1),
+                        )
+                    nc.scalar.activation(out=sq[:, a, :], in_=w_ps[a][:], func=ACT.Square)
+                rstd = column_rstd(sq)
+                y = back.tile([P, CB, T], F32, name="y")
+                sq = ring.tile([P, CB, W], BF16, name="sq")
+                for a in range(CB):
+                    nc.vector.tensor_tensor(out=y[:, a, :], in0=w_ps[a][:], in1=rstd[:], op=ALU.mult)
+                    nc.scalar.activation(out=sq[:, a, :], in_=y[:, a, :], func=ACT.Square, bias=l_c[:, a : a + 1])
+                rstd = column_rstd(sq)
+                for a in range(CB):
+                    res = ring.tile([P, T], F32, name="res")
+                    nc.vector.scalar_tensor_tensor(
+                        out=res[:], in0=y[:, a, :], scalar=l_c[:, a : a + 1], in1=rstd[:], op0=ALU.add, op1=ALU.mult
+                    )
+                    nc.sync.dma_start(out[a * P : (a + 1) * P, tok], res[:])
+
+            heads = [(b, h) for b in range(B) for h in range(NH)]
+            a_t_next = scores(*heads[0])
+            for i in range(len(heads) + 2):
+                if i < len(heads):
+                    a_t_now = a_t_next
+                    if i + 1 < len(heads):
+                        a_t_next = scores(*heads[i + 1])
+                    made = values(heads[i][0], a_t_now)
+                if 1 <= i <= len(heads):
+                    gate(*heads[i - 1], *made_before)
+                if i >= 2 and heads[i - 2][1] == NH - 1:
+                    block_output(heads[i - 2][0])
+                made_before = made

@@ -42,6 +42,8 @@ def tile_bdhhrm_b_kernel(tc, table, h_init, l_init, enc, enc_v, dec, cos_t, sin_
         nc.vector.memset(eps_t[:], EPS)
         ident = held.tile([P, P], BF16, name="ident")
         make_identity(nc, ident[:])
+        ident32 = held.tile([P, P], F32, name="ident32")
+        make_identity(nc, ident32[:])
         later = held.tile([P, P], F32, name="later")
         nc.gpsimd.memset(later[:], 1.0)
         nc.gpsimd.affine_select(
@@ -50,8 +52,9 @@ def tile_bdhhrm_b_kernel(tc, table, h_init, l_init, enc, enc_v, dec, cos_t, sin_
 
         def column_rstd(squares):
             q_ps = bank()
-            for a in range(CB):
-                nc.tensor.matmul(q_ps[:], lhsT=mean_w16[:], rhs=squares[:, a, :], start=(a == 0), stop=(a == CB - 1))
+            blocks = squares.shape[1]
+            for a in range(blocks):
+                nc.tensor.matmul(q_ps[:], lhsT=mean_w16[:], rhs=squares[:, a, :], start=(a == 0), stop=(a == blocks - 1))
             rstd = ring.tile([P, W], F32, name="rstd")
             nc.scalar.activation(out=rstd[:], in_=q_ps[:], func=ACT.Abs_reciprocal_sqrt, bias=eps_t[:, 0:1])
             return rstd
@@ -66,25 +69,55 @@ def tile_bdhhrm_b_kernel(tc, table, h_init, l_init, enc, enc_v, dec, cos_t, sin_
         xi_t = [held.tile([P, C], BF16, name=f"xi_t{j}") for j in range(N // P)]
         enc_sb = held.tile([P, CB, HN], BF16, name="enc_sb")
         ev_sb = held.tile([P, CB, HN], BF16, name="ev_sb")
-        dec_sb = held.tile([P, KB, C], BF16, name="dec_sb")
         cos_q = held.tile([P, 2, T], BF16, name="cos_q")
         sin_x = held.tile([P, 2, T], BF16, name="sin_x")
 
-        with tc.tile_pool(name="front", bufs=1) as front:
-            tn = [front.tile([P, S], F32, name=f"tn{a}") for a in range(CB)]
-            for s in range(S // W):
+        xs = held.tile([P, KB, N], BF16, name="xs")
+        qr = held.tile([P, KB, N], BF16, name="qr")
+        gated = held.tile([P, KB, N], BF16, name="gated")
+        dec_c = held.tile([P, KB, C], BF16, name="dec_c")
+
+        def rows_of(h, e):
+            return slice(h * NS + e, (h + 1) * NS, 2)
+
+        def codes(b):
+            tok = slice(b * T, (b + 1) * T)
+            for k0 in range(0, KB, 4):
+                x_ps = [bank() for k in range(4)]
                 for a in range(CB):
-                    nc.sync.dma_start(tn[a][:, s * W : (s + 1) * W], table[a * P : (a + 1) * P, s * W : (s + 1) * W])
+                    for k in range(4):
+                        nc.tensor.matmul(
+                            x_ps[k][:],
+                            lhsT=enc_sb[:, a, rows_of((k0 + k) // 2, k % 2)],
+                            rhs=xi[a][:, tok],
+                            start=(a == 0),
+                            stop=(a == CB - 1),
+                        )
+                for k in range(4):
+                    nc.scalar.activation(out=xs[:, k0 + k, tok], in_=x_ps[k][:], func=ACT.Relu)
+
+        def rotate(b, h):
+            tok = slice(b * T, (b + 1) * T)
+            own = pair.tile([P, 2, T], BF16, name="own")
+            other = pair.tile([P, 2, T], BF16, name="other")
+            nc.vector.tensor_tensor(out=own[:], in0=xs[:, 2 * h : 2 * h + 2, tok], in1=cos_q[:], op=ALU.mult)
+            nc.vector.tensor_tensor(out=other[:], in0=xs[:, 2 * h : 2 * h + 2, tok], in1=sin_x[:], op=ALU.mult)
+            for e in range(2):
+                nc.vector.tensor_tensor(out=qr[:, 2 * h + e, tok], in0=own[:, e, :], in1=other[:, 1 - e, :], op=ALU.add)
+
+        with tc.tile_pool(name="front", bufs=1) as front:
+
+            def piece_tile():
+                return front.tile([P, CB, W], F32, name="piece", tag="piece", bufs=4)
+
+            pieces = S // W
+            raw = []
+            for s in range(pieces):
+                raw.append(piece_tile())
+                for a in range(CB):
+                    nc.sync.dma_start(raw[s][:, a, :], table[a * P : (a + 1) * P, s * W : (s + 1) * W])
             nc.sync.dma_start(enc_sb[:], enc.rearrange("(a p) k -> p a k", p=P))
-            cos_raw = front.tile([P, 2, T], F32, name="cos_raw")
-            sin_raw = front.tile([P, 2, T], F32, name="sin_raw")
-            nc.sync.dma_start(cos_raw[:], cos_t.rearrange("(p e) t -> p e t", e=2))
-            nc.sync.dma_start(sin_raw[:], sin_t.rearrange("(p e) t -> p e t", e=2))
             nc.sync.dma_start(ev_sb[:], enc_v.rearrange("(a p) k -> p a k", p=P))
-            for h in range(NH):
-                nc.sync.dma_start(
-                    dec_sb[:, 2 * h : 2 * h + 2, :], dec[h * NS : (h + 1) * NS, :].rearrange("(p e) c -> p e c", e=2)
-                )
 
             both = held.tile([P, 2 * CB], F32, name="both")
             nc.vector.tensor_tensor(out=both[:, 0:CB], in0=h_t[:], in1=l_t[:], op=ALU.add)
@@ -108,87 +141,83 @@ def tile_bdhhrm_b_kernel(tc, table, h_init, l_init, enc, enc_v, dec, cos_t, sin_
             for a in range(CB):
                 nc.vector.tensor_copy(z0_wide[a][:], z0_c[:, a : a + 1].to_broadcast([P, W]))
 
-            def mean_of(s):
-                cols = slice(s * W, (s + 1) * W)
-                m_ps = bank()
-                for a in range(CB):
-                    nc.tensor.matmul(m_ps[:], lhsT=mean_w32[:], rhs=tn[a][:, cols], start=(a == 0), stop=(a == CB - 1))
-                return m_ps
+            tn = [front.tile([P, S], F32, name=f"tn{a}") for a in range(CB)]
+            groups = W // P
 
-            def centre(s, m_ps):
-                cols = slice(s * W, (s + 1) * W)
+            def normalise(s):
+                flipped = []
+                for g in range(groups):
+                    f_ps = bank()
+                    for a in range(CB):
+                        nc.tensor.transpose(f_ps[:, a * P : (a + 1) * P], raw[s][:, a, g * P : (g + 1) * P], ident32[:])
+                    stats = ring.tile([P, 6], F32, name="stats")
+                    nc.vector.bn_stats(out=stats[:], in_=f_ps[:])
+                    mean_var = ring.tile([P, 2], F32, name="mean_var")
+                    nc.vector.bn_aggr(out=mean_var[:], in_=stats[:])
+                    neg_m = ring.tile([P, 1], F32, name="neg_m")
+                    nc.vector.tensor_scalar(out=neg_m[:], in0=mean_var[:, 0:1], scalar1=-1.0, scalar2=None, op0=ALU.mult)
+                    factor = ring.tile([P, 1], F32, name="factor")
+                    nc.scalar.activation(
+                        out=factor[:], in_=mean_var[:, 1:2], func=ACT.Abs_reciprocal_sqrt, bias=eps_t[:, 0:1]
+                    )
+                    shift = ring.tile([P, 1], F32, name="shift")
+                    nc.scalar.activation(out=shift[:], in_=factor[:], func=ACT.Identity, scale=neg_m[:, 0:1])
+                    words = front.tile([P, C], F32, name="words", bufs=2 * groups)
+                    nc.scalar.activation(
+                        out=words[:], in_=f_ps[:], func=ACT.Identity, scale=factor[:, 0:1], bias=shift[:, 0:1]
+                    )
+                    flipped.append(words)
+                return flipped
+
+            def flip_back(s, flipped):
+                for a in range(CB):
+                    b_ps = bank()
+                    for g in range(groups):
+                        nc.tensor.transpose(b_ps[:, g * P : (g + 1) * P], flipped[g][:, a * P : (a + 1) * P], ident32[:])
+                    if a % 2 == 0:
+                        nc.vector.tensor_copy(tn[a][:, s * W : (s + 1) * W], b_ps[:])
+                    else:
+                        nc.scalar.copy(out=tn[a][:, s * W : (s + 1) * W], in_=b_ps[:])
+
+            flipped_next = normalise(0)
+            for s in range(pieces):
+                flipped_now = flipped_next
+                if s + 1 < pieces:
+                    flipped_next = normalise(s + 1)
+                flip_back(s, flipped_now)
+
+            rotary = piece_tile()
+            nc.sync.dma_start(rotary[:, 0:2, :], cos_t.rearrange("(p e) t -> p e t", e=2))
+            nc.sync.dma_start(rotary[:, 2:4, :], sin_t.rearrange("(p e) t -> p e t", e=2))
+
+            nc.gpsimd.tensor_scalar(out=cos_q[:], in0=rotary[:, 0:2, :], scalar1=0.25, scalar2=0.0, op0=ALU.mult, op1=ALU.add)
+            for e in range(2):
+                nc.gpsimd.tensor_scalar(
+                    out=sin_x[:, e, :], in0=rotary[:, 3 - e, :], scalar1=0.25, scalar2=0.0, op0=ALU.mult, op1=ALU.add
+                )
+
+            def look_up(b):
+                u_c = piece_tile()
                 sq = ring.tile([P, CB, W], BF16, name="sq")
                 for a in range(CB):
-                    nc.vector.tensor_tensor(out=tn[a][:, cols], in0=tn[a][:, cols], in1=m_ps[:], op=ALU.subtract)
-                    nc.scalar.activation(out=sq[:, a, :], in_=tn[a][:, cols], func=ACT.Square)
-                return column_rstd(sq)
-
-            def scale(s, rstd):
-                cols = slice(s * W, (s + 1) * W)
-                for a in range(CB):
-                    nc.vector.tensor_tensor(out=tn[a][:, cols], in0=tn[a][:, cols], in1=rstd[:], op=ALU.mult)
-
-            pieces = S // W
-            m_next = mean_of(0)
-            for s in range(pieces):
-                m_now = m_next
-                if s + 1 < pieces:
-                    m_next = mean_of(s + 1)
-                rstd_now = centre(s, m_now)
-                if s > 0:
-                    scale(s - 1, rstd_before)
-                rstd_before = rstd_now
-            scale(pieces - 1, rstd_before)
-
-            u_c = [front.tile([P, N], F32, name=f"u_c{a}") for a in range(CB)]
-            for b in range(B):
-                for a in range(CB):
                     nc.vector.tensor_tensor(
-                        out=u_c[a][:, b * T : (b + 1) * T],
+                        out=u_c[:, a, :],
                         in0=tn[a][:].indirect(offsets[:, b * (T // 16) : (b + 1) * (T // 16)]),
                         in1=z0_wide[a][:],
                         op=ALU.add,
                     )
-            for b in range(B):
-                tok = slice(b * T, (b + 1) * T)
-                sq = ring.tile([P, CB, W], BF16, name="sq")
-                for a in range(CB):
-                    nc.scalar.activation(out=sq[:, a, :], in_=u_c[a][:, tok], func=ACT.Square)
+                    nc.scalar.activation(out=sq[:, a, :], in_=u_c[:, a, :], func=ACT.Square)
+                return u_c, sq
+
+            def norm_of_u(b, u_c, sq):
                 rstd = column_rstd(sq)
                 for a in range(CB):
-                    nc.vector.tensor_tensor(out=xi[a][:, tok], in0=u_c[a][:, tok], in1=rstd[:], op=ALU.mult)
+                    nc.vector.tensor_tensor(out=xi[a][:, b * T : (b + 1) * T], in0=u_c[:, a, :], in1=rstd[:], op=ALU.mult)
 
-            nc.gpsimd.tensor_scalar(out=cos_q[:], in0=cos_raw[:], scalar1=0.25, scalar2=None, op0=ALU.mult)
-            for e in range(2):
-                nc.gpsimd.tensor_scalar(
-                    out=sin_x[:, e, :], in0=sin_raw[:, 1 - e, :], scalar1=0.25, scalar2=None, op0=ALU.mult
-                )
-
-        xs = held.tile([P, KB, N], BF16, name="xs")
-        qr = held.tile([P, KB, N], BF16, name="qr")
-        gated = held.tile([P, KB, N], BF16, name="gated")
-
-        def rows_of(h, e):
-            return slice(h * NS + e, (h + 1) * NS, 2)
-
-        def codes(b):
-            tok = slice(b * T, (b + 1) * T)
-            for h in range(NH):
-                for e in range(2):
-                    x_ps = bank()
-                    for a in range(CB):
-                        nc.tensor.matmul(
-                            x_ps[:], lhsT=enc_sb[:, a, rows_of(h, e)], rhs=xi[a][:, tok], start=(a == 0), stop=(a == CB - 1)
-                        )
-                    nc.scalar.activation(out=xs[:, 2 * h + e, tok], in_=x_ps[:], func=ACT.Relu)
-                own = pair.tile([P, 2, T], BF16, name="own")
-                other = pair.tile([P, 2, T], BF16, name="other")
-                nc.vector.tensor_tensor(out=own[:], in0=xs[:, 2 * h : 2 * h + 2, tok], in1=cos_q[:], op=ALU.mult)
-                nc.vector.tensor_tensor(out=other[:], in0=xs[:, 2 * h : 2 * h + 2, tok], in1=sin_x[:], op=ALU.mult)
-                for e in range(2):
-                    nc.vector.tensor_tensor(out=qr[:, 2 * h + e, tok], in0=own[:, e, :], in1=other[:, 1 - e, :], op=ALU.add)
-
-        codes(0)
+            norm_of_u(0, *look_up(0))
+            looked_up = look_up(1)
+            codes(0)
+            norm_of_u(1, *looked_up)
 
         for j in range(N // P):
             t_ps = bank((P, C), BF16)
@@ -196,20 +225,24 @@ def tile_bdhhrm_b_kernel(tc, table, h_init, l_init, enc, enc_v, dec, cos_t, sin_
                 nc.tensor.transpose(t_ps[:, a * P : (a + 1) * P], xi[a][:, j * P : (j + 1) * P], ident[:])
             nc.scalar.copy(out=xi_t[j][:], in_=t_ps[:])
 
-        dec_c = held.tile([P, KB, C], BF16, name="dec_c")
-        neg_mean = held.tile([P, KB], F32, name="neg_mean")
-        for k in range(KB):
-            unused = pair.tile([P, C], BF16, name="unused")
-            nc.scalar.activation(
-                out=unused[:], in_=dec_sb[:, k, :], func=ACT.Copy, scale=-1.0 / C, accum_out=neg_mean[:, k : k + 1]
-            )
-            nc.gpsimd.tensor_scalar(
-                out=dec_c[:, k, :], in0=dec_sb[:, k, :], scalar1=neg_mean[:, k : k + 1], scalar2=None, op0=ALU.add
-            )
-
         codes(1)
 
         with tc.tile_pool(name="back", bufs=2) as back:
+            dec_sb = back.tile([P, KB, C], BF16, name="dec_sb", bufs=1)
+            for h in range(NH):
+                nc.sync.dma_start(
+                    dec_sb[:, 2 * h : 2 * h + 2, :], dec[h * NS : (h + 1) * NS, :].rearrange("(p e) c -> p e c", e=2)
+                )
+            neg_mean = held.tile([P, KB], F32, name="neg_mean")
+            for k in range(KB):
+                unused = pair.tile([P, C], BF16, name="unused")
+                nc.scalar.activation(
+                    out=unused[:], in_=dec_sb[:, k, :], func=ACT.Copy, scale=-1.0 / C, accum_out=neg_mean[:, k : k + 1]
+                )
+                nc.gpsimd.tensor_scalar(
+                    out=dec_c[:, k, :], in0=dec_sb[:, k, :], scalar1=1.0, scalar2=neg_mean[:, k : k + 1], op0=ALU.mult, op1=ALU.add
+                )
+
             def scores(b, h):
                 a_t = back.tile([P, RB, T], BF16, name="a_t")
                 for i in range(RB):
@@ -241,38 +274,45 @@ def tile_bdhhrm_b_kernel(tc, table, h_init, l_init, enc, enc_v, dec, cos_t, sin_
                             start=(i == 0),
                             stop=(i == RB - 1),
                         )
+                    nc.scalar.copy(out=av[:, a, :], in_=av_ps[:])
                     nc.scalar.activation(out=sq[:, a, :], in_=av_ps[:], func=ACT.Square)
-                    nc.vector.tensor_copy(av[:, a, :], av_ps[:])
-                return av, sq
+                halves = pair.tile([P, 2, W], BF16, name="halves")
+                nc.vector.tensor_tensor(out=halves[:], in0=sq[:, 0:2, :], in1=sq[:, 2:4, :], op=ALU.add)
+                whole = pair.tile([P, 1, W], BF16, name="whole")
+                nc.vector.tensor_tensor(out=whole[:, 0, :], in0=halves[:, 0, :], in1=halves[:, 1, :], op=ALU.add)
+                return av, whole
 
-            def gate(b, h, av, sq):
+            def gate(b, h, av, squares):
                 tok = slice(b * T, (b + 1) * T)
-                rstd = column_rstd(sq)
+                prod = pair.tile([P, 2, T], F32, name="prod")
                 for e in range(2):
                     v_ps = bank()
                     for a in range(CB):
                         nc.tensor.matmul(
                             v_ps[:], lhsT=ev_sb[:, a, rows_of(h, e)], rhs=av[:, a, :], start=(a == 0), stop=(a == CB - 1)
                         )
-                    prod = pair.tile([P, T], F32, name="prod")
                     nc.vector.scalar_tensor_tensor(
-                        out=prod[:], in0=v_ps[:], scalar=0.0, in1=xs[:, 2 * h + e, tok], op0=ALU.max, op1=ALU.mult
+                        out=prod[:, e, :], in0=v_ps[:], scalar=0.0, in1=xs[:, 2 * h + e, tok], op0=ALU.max, op1=ALU.mult
                     )
-                    nc.gpsimd.tensor_tensor(out=gated[:, 2 * h + e, tok], in0=prod[:], in1=rstd[:], op=ALU.mult)
+                rstd = column_rstd(squares)
+                for e in range(2):
+                    nc.vector.tensor_tensor(out=gated[:, 2 * h + e, tok], in0=prod[:, e, :], in1=rstd[:], op=ALU.mult)
 
-            def block_output(b):
+            def project(b):
                 tok = slice(b * T, (b + 1) * T)
                 w_ps = [bank() for a in range(CB)]
+                for blocks in (range(0, KB - 2), range(KB - 2, KB)):
+                    for a in range(CB):
+                        for k in blocks:
+                            nc.tensor.matmul(
+                                w_ps[a][:],
+                                lhsT=dec_c[:, k, a * P : (a + 1) * P],
+                                rhs=gated[:, k, tok],
+                                start=(k == 0),
+                                stop=(k == KB - 1),
+                            )
                 sq = ring.tile([P, CB, W], BF16, name="sq")
                 for a in range(CB):
-                    for k in range(KB):
-                        nc.tensor.matmul(
-                            w_ps[a][:],
-                            lhsT=dec_c[:, k, a * P : (a + 1) * P],
-                            rhs=gated[:, k, tok],
-                            start=(k == 0),
-                            stop=(k == KB - 1),
-                        )
                     nc.scalar.activation(out=sq[:, a, :], in_=w_ps[a][:], func=ACT.Square)
                 rstd = column_rstd(sq)
                 y = back.tile([P, CB, T], F32, name="y")
@@ -280,24 +320,35 @@ def tile_bdhhrm_b_kernel(tc, table, h_init, l_init, enc, enc_v, dec, cos_t, sin_
                 for a in range(CB):
                     nc.vector.tensor_tensor(out=y[:, a, :], in0=w_ps[a][:], in1=rstd[:], op=ALU.mult)
                     nc.scalar.activation(out=sq[:, a, :], in_=y[:, a, :], func=ACT.Square, bias=l_c[:, a : a + 1])
+                return y, sq
+
+            def finish(b, y, sq):
+                tok = slice(b * T, (b + 1) * T)
                 rstd = column_rstd(sq)
+                res = back.tile([P, CB, T], F32, name="res")
                 for a in range(CB):
-                    res = ring.tile([P, T], F32, name="res")
                     nc.vector.scalar_tensor_tensor(
-                        out=res[:], in0=y[:, a, :], scalar=l_c[:, a : a + 1], in1=rstd[:], op0=ALU.add, op1=ALU.mult
+                        out=res[:, a, :], in0=y[:, a, :], scalar=l_c[:, a : a + 1], in1=rstd[:], op0=ALU.add, op1=ALU.mult
                     )
-                    nc.sync.dma_start(out[a * P : (a + 1) * P, tok], res[:])
+                    nc.sync.dma_start(out[a * P : (a + 1) * P, tok], res[:, a, :])
 
             heads = [(b, h) for b in range(B) for h in range(NH)]
-            a_t_next = scores(*heads[0])
-            for i in range(len(heads) + 2):
-                if i < len(heads):
-                    a_t_now = a_t_next
-                    if i + 1 < len(heads):
-                        a_t_next = scores(*heads[i + 1])
-                    made = values(heads[i][0], a_t_now)
-                if 1 <= i <= len(heads):
-                    gate(*heads[i - 1], *made_before)
-                if i >= 2 and heads[i - 2][1] == NH - 1:
-                    block_output(heads[i - 2][0])
-                made_before = made
+            count = len(heads)
+            rotate(*heads[0])
+            rotate(*heads[1])
+            a_t_of = {0: scores(*heads[0])}
+            made_of = {}
+            normed_of = {}
+            for i in range(count + 3):
+                if i + 2 < count:
+                    rotate(*heads[i + 2])
+                if i + 1 < count:
+                    a_t_of[i + 1] = scores(*heads[i + 1])
+                if i < count:
+                    made_of[i] = values(heads[i][0], a_t_of[i])
+                if 0 <= i - 1 < count:
+                    gate(*heads[i - 1], *made_of[i - 1])
+                if 0 <= i - 2 < count and heads[i - 2][1] == NH - 1:
+                    normed_of[i - 2] = project(heads[i - 2][0])
+                if 0 <= i - 3 < count and heads[i - 3][1] == NH - 1:
+                    finish(heads[i - 3][0], *normed_of[i - 3])

@@ -15,6 +15,7 @@ KB = HN // P
 RB = T // P
 W = 512
 EPS = 1e-5
+HALVES = (slice(0, T // 2), slice(T // 2, T))
 
 FLOPS = 2 * (C * HN * N + B * NH * (NS + C) * (T * (T - 1) // 2) + C * HN * N + HN * C * N)
 
@@ -51,11 +52,11 @@ def tile_bdhhrm_b_kernel(tc, table, h_init, l_init, enc, enc_v, dec, cos_t, sin_
         )
 
         def column_rstd(squares):
-            q_ps = bank()
-            blocks = squares.shape[1]
+            blocks, width = squares.shape[1], squares.shape[2]
+            q_ps = bank((P, width))
             for a in range(blocks):
                 nc.tensor.matmul(q_ps[:], lhsT=mean_w16[:], rhs=squares[:, a, :], start=(a == 0), stop=(a == blocks - 1))
-            rstd = ring.tile([P, W], F32, name="rstd")
+            rstd = ring.tile([P, width], F32, name="rstd")
             nc.scalar.activation(out=rstd[:], in_=q_ps[:], func=ACT.Abs_reciprocal_sqrt, bias=eps_t[:, 0:1])
             return rstd
 
@@ -311,26 +312,32 @@ def tile_bdhhrm_b_kernel(tc, table, h_init, l_init, enc, enc_v, dec, cos_t, sin_
                                 start=(k == 0),
                                 stop=(k == KB - 1),
                             )
-                sq = ring.tile([P, CB, W], BF16, name="sq")
-                for a in range(CB):
-                    nc.scalar.activation(out=sq[:, a, :], in_=w_ps[a][:], func=ACT.Square)
-                rstd = column_rstd(sq)
                 y = back.tile([P, CB, T], F32, name="y")
-                sq = ring.tile([P, CB, W], BF16, name="sq")
-                for a in range(CB):
-                    nc.vector.tensor_tensor(out=y[:, a, :], in0=w_ps[a][:], in1=rstd[:], op=ALU.mult)
-                    nc.scalar.activation(out=sq[:, a, :], in_=y[:, a, :], func=ACT.Square, bias=l_c[:, a : a + 1])
-                return y, sq
+                squares = []
+                for half in HALVES:
+                    sq = ring.tile([P, CB, T // 2], BF16, name="sq_half")
+                    for a in range(CB):
+                        nc.scalar.activation(out=sq[:, a, :], in_=w_ps[a][:, half], func=ACT.Square)
+                    squares.append(sq)
+                for half, sq_w in zip(HALVES, squares):
+                    rstd = column_rstd(sq_w)
+                    sq = ring.tile([P, CB, T // 2], BF16, name="sq_half")
+                    for a in range(CB):
+                        nc.vector.tensor_tensor(out=y[:, a, half], in0=w_ps[a][:, half], in1=rstd[:], op=ALU.mult)
+                        nc.scalar.activation(out=sq[:, a, :], in_=y[:, a, half], func=ACT.Square, bias=l_c[:, a : a + 1])
+                    squares.append(sq)
+                return y, squares[2:]
 
-            def finish(b, y, sq):
-                tok = slice(b * T, (b + 1) * T)
-                rstd = column_rstd(sq)
+            def finish(b, y, squares):
                 res = back.tile([P, CB, T], F32, name="res")
+                for half, sq in zip(HALVES, squares):
+                    rstd = column_rstd(sq)
+                    for a in range(CB):
+                        nc.vector.scalar_tensor_tensor(
+                            out=res[:, a, half], in0=y[:, a, half], scalar=l_c[:, a : a + 1], in1=rstd[:], op0=ALU.add, op1=ALU.mult
+                        )
                 for a in range(CB):
-                    nc.vector.scalar_tensor_tensor(
-                        out=res[:, a, :], in0=y[:, a, :], scalar=l_c[:, a : a + 1], in1=rstd[:], op0=ALU.add, op1=ALU.mult
-                    )
-                    nc.sync.dma_start(out[a * P : (a + 1) * P, tok], res[:, a, :])
+                    nc.sync.dma_start(out[a * P : (a + 1) * P, b * T : (b + 1) * T], res[:, a, :])
 
             heads = [(b, h) for b in range(B) for h in range(NH)]
             count = len(heads)

@@ -26,7 +26,7 @@ def tile_bdhhrm_b_kernel(tc, table, h_init, l_init, enc, enc_v, dec, cos_t, sin_
         tc.tile_pool(name="held", bufs=1) as held,
         tc.tile_pool(name="pair", bufs=2) as pair,
         tc.tile_pool(name="ring", bufs=3) as ring,
-        tc.psum_pool(name="psum", bufs=8) as psum,
+        tc.psum_pool(name="psum", bufs=7) as psum,
     ):
 
         def bank(shape=(P, W), dtype=F32):
@@ -41,8 +41,6 @@ def tile_bdhhrm_b_kernel(tc, table, h_init, l_init, enc, enc_v, dec, cos_t, sin_
         nc.vector.memset(mean_w16[:], 1.0 / C)
         eps_t = held.tile([P, 1], F32, name="eps_t")
         nc.vector.memset(eps_t[:], EPS)
-        ident = held.tile([P, P], BF16, name="ident")
-        make_identity(nc, ident[:])
         ident32 = held.tile([P, P], F32, name="ident32")
         make_identity(nc, ident32[:])
         later = held.tile([P, P], F32, name="later")
@@ -53,7 +51,7 @@ def tile_bdhhrm_b_kernel(tc, table, h_init, l_init, enc, enc_v, dec, cos_t, sin_
 
         def column_rstd(squares):
             blocks, width = squares.shape[1], squares.shape[2]
-            q_ps = bank((P, width))
+            q_ps = psum.tile([P, width], F32, name="q_ps", tag="sums", bufs=1)
             for a in range(blocks):
                 nc.tensor.matmul(q_ps[:], lhsT=mean_w16[:], rhs=squares[:, a, :], start=(a == 0), stop=(a == blocks - 1))
             rstd = ring.tile([P, width], F32, name="rstd")
@@ -66,7 +64,7 @@ def tile_bdhhrm_b_kernel(tc, table, h_init, l_init, enc, enc_v, dec, cos_t, sin_
             nc.scalar.dma_start(h_t[:], h_init.rearrange("(a p) o -> p (a o)", p=P))
             nc.scalar.dma_start(l_t[:], l_init.rearrange("(a p) o -> p (a o)", p=P))
 
-        xi = [held.tile([P, N], BF16, name=f"xi{a}") for a in range(CB)]
+        u16 = [held.tile([P, N], BF16, name=f"u16_{a}") for a in range(CB)]
         xi_t = [held.tile([P, C], BF16, name=f"xi_t{j}") for j in range(N // P)]
         enc_sb = held.tile([P, CB, HN], BF16, name="enc_sb")
         ev_sb = held.tile([P, CB, HN], BF16, name="ev_sb")
@@ -81,21 +79,24 @@ def tile_bdhhrm_b_kernel(tc, table, h_init, l_init, enc, enc_v, dec, cos_t, sin_
         def rows_of(h, e):
             return slice(h * NS + e, (h + 1) * NS, 2)
 
-        def codes(b):
-            tok = slice(b * T, (b + 1) * T)
-            for k0 in range(0, KB, 4):
-                x_ps = [bank() for k in range(4)]
-                for a in range(CB):
-                    for k in range(4):
-                        nc.tensor.matmul(
-                            x_ps[k][:],
-                            lhsT=enc_sb[:, a, rows_of((k0 + k) // 2, k % 2)],
-                            rhs=xi[a][:, tok],
-                            start=(a == 0),
-                            stop=(a == CB - 1),
-                        )
+        def code_sums(b, k0):
+            x_ps = [bank() for k in range(4)]
+            for a in range(CB):
                 for k in range(4):
-                    nc.scalar.activation(out=xs[:, k0 + k, tok], in_=x_ps[k][:], func=ACT.Relu)
+                    nc.tensor.matmul(
+                        x_ps[k][:],
+                        lhsT=enc_sb[:, a, rows_of((k0 + k) // 2, k % 2)],
+                        rhs=u16[a][:, b * T : (b + 1) * T],
+                        start=(a == 0),
+                        stop=(a == CB - 1),
+                    )
+            return x_ps
+
+        def keep_codes(b, k0, x_ps, rstd):
+            for k in range(4):
+                nc.vector.scalar_tensor_tensor(
+                    out=xs[:, k0 + k, b * T : (b + 1) * T], in0=x_ps[k][:], scalar=0.0, in1=rstd[:], op0=ALU.max, op1=ALU.mult
+                )
 
         def rotate(b, h):
             tok = slice(b * T, (b + 1) * T)
@@ -207,43 +208,63 @@ def tile_bdhhrm_b_kernel(tc, table, h_init, l_init, enc, enc_v, dec, cos_t, sin_
                         in1=z0_wide[a][:],
                         op=ALU.add,
                     )
+                    nc.scalar.copy(out=u16[a][:, b * T : (b + 1) * T], in_=u_c[:, a, :])
                     nc.scalar.activation(out=sq[:, a, :], in_=u_c[:, a, :], func=ACT.Square)
                 return u_c, sq
 
-            def norm_of_u(b, u_c, sq):
+            def token_rstd(sq):
+                q_ps = psum.tile([P, RB], F32, name="q_ps", tag="sums", bufs=1)
+                for i in range(RB):
+                    for a in range(CB):
+                        nc.tensor.matmul(
+                            q_ps[:, i : i + 1],
+                            lhsT=sq[:, a, i * P : (i + 1) * P],
+                            rhs=mean_w16[:, 0:1],
+                            start=(a == 0),
+                            stop=(a == CB - 1),
+                        )
+                rstd = pair.tile([P, RB], F32, name="rstd_tok")
+                nc.scalar.activation(out=rstd[:], in_=q_ps[:], func=ACT.Abs_reciprocal_sqrt, bias=eps_t[:, 0:1])
+                return rstd
+
+            looked_up = [look_up(b) for b in range(B)]
+            for b in range(B):
+                u_c, sq = looked_up[b]
+                x_ps = code_sums(b, 0)
                 rstd = column_rstd(sq)
-                for a in range(CB):
-                    nc.vector.tensor_tensor(out=xi[a][:, b * T : (b + 1) * T], in0=u_c[:, a, :], in1=rstd[:], op=ALU.mult)
+                keep_codes(b, 0, x_ps, rstd)
+                keep_codes(b, 4, code_sums(b, 4), rstd)
+                rstd_tok = token_rstd(sq)
+                for i in range(RB):
+                    t_ps = bank()
+                    for a in range(CB):
+                        nc.tensor.transpose(t_ps[:, a * P : (a + 1) * P], u_c[:, a, i * P : (i + 1) * P], ident32[:])
+                    nc.scalar.activation(out=xi_t[b * RB + i][:], in_=t_ps[:], func=ACT.Identity, scale=rstd_tok[:, i : i + 1])
 
-            norm_of_u(0, *look_up(0))
-            looked_up = look_up(1)
-            codes(0)
-            norm_of_u(1, *looked_up)
-
-        for j in range(N // P):
-            t_ps = bank((P, C), BF16)
-            for a in range(CB):
-                nc.tensor.transpose(t_ps[:, a * P : (a + 1) * P], xi[a][:, j * P : (j + 1) * P], ident[:])
-            nc.scalar.copy(out=xi_t[j][:], in_=t_ps[:])
-
-        codes(1)
+            neg_mean = held.tile([P, KB], F32, name="neg_mean")
+            for h in range(NH):
+                dec_rows = looked_up[0][0][:, h, :].bitcast(BF16)
+                nc.sync.dma_start(dec_rows, dec[h * NS : (h + 1) * NS, :].rearrange("(p e) c -> p (e c)", e=2))
+                for e in range(2):
+                    k = 2 * h + e
+                    unused = pair.tile([P, C], BF16, name="unused")
+                    nc.scalar.activation(
+                        out=unused[:],
+                        in_=dec_rows[:, e * C : (e + 1) * C],
+                        func=ACT.Copy,
+                        scale=-1.0 / C,
+                        accum_out=neg_mean[:, k : k + 1],
+                    )
+                    nc.gpsimd.tensor_scalar(
+                        out=dec_c[:, k, :],
+                        in0=dec_rows[:, e * C : (e + 1) * C],
+                        scalar1=1.0,
+                        scalar2=neg_mean[:, k : k + 1],
+                        op0=ALU.mult,
+                        op1=ALU.add,
+                    )
 
         with tc.tile_pool(name="back", bufs=2) as back:
-            dec_sb = back.tile([P, KB, C], BF16, name="dec_sb", bufs=1)
-            for h in range(NH):
-                nc.sync.dma_start(
-                    dec_sb[:, 2 * h : 2 * h + 2, :], dec[h * NS : (h + 1) * NS, :].rearrange("(p e) c -> p e c", e=2)
-                )
-            neg_mean = held.tile([P, KB], F32, name="neg_mean")
-            for k in range(KB):
-                unused = pair.tile([P, C], BF16, name="unused")
-                nc.scalar.activation(
-                    out=unused[:], in_=dec_sb[:, k, :], func=ACT.Copy, scale=-1.0 / C, accum_out=neg_mean[:, k : k + 1]
-                )
-                nc.gpsimd.tensor_scalar(
-                    out=dec_c[:, k, :], in0=dec_sb[:, k, :], scalar1=1.0, scalar2=neg_mean[:, k : k + 1], op0=ALU.mult, op1=ALU.add
-                )
-
             def scores(b, h):
                 a_t = back.tile([P, RB, T], BF16, name="a_t")
                 for i in range(RB):

@@ -43,6 +43,8 @@ def tile_bdhhrm_b_kernel(tc, table, h_init, l_init, enc, enc_v, dec, cos_t, sin_
         nc.vector.memset(eps_t[:], EPS)
         ident32 = held.tile([P, P], F32, name="ident32")
         make_identity(nc, ident32[:])
+        ident16 = held.tile([P, P], BF16, name="ident16")
+        make_identity(nc, ident16[:])
         later = held.tile([P, P], F32, name="later")
         nc.gpsimd.memset(later[:], 1.0)
         nc.gpsimd.affine_select(
@@ -65,7 +67,8 @@ def tile_bdhhrm_b_kernel(tc, table, h_init, l_init, enc, enc_v, dec, cos_t, sin_
             nc.scalar.dma_start(l_t[:], l_init.rearrange("(a p) o -> p (a o)", p=P))
 
         u16 = [held.tile([P, N], BF16, name=f"u16_{a}") for a in range(CB)]
-        xi_t = [held.tile([P, C], BF16, name=f"xi_t{j}") for j in range(N // P)]
+        u_t = [held.tile([P, C], BF16, name=f"u_t{j}") for j in range(N // P)]
+        rstd_tok = [held.tile([P, RB], F32, name=f"rstd_tok{b}") for b in range(B)]
         enc_sb = held.tile([P, CB, HN], BF16, name="enc_sb")
         ev_sb = held.tile([P, CB, HN], BF16, name="ev_sb")
         cos_q = held.tile([P, 2, T], BF16, name="cos_q")
@@ -212,7 +215,7 @@ def tile_bdhhrm_b_kernel(tc, table, h_init, l_init, enc, enc_v, dec, cos_t, sin_
                     nc.scalar.activation(out=sq[:, a, :], in_=u_c[:, a, :], func=ACT.Square)
                 return u_c, sq
 
-            def token_rstd(sq):
+            def token_rstd(b, sq):
                 q_ps = psum.tile([P, RB], F32, name="q_ps", tag="sums", bufs=1)
                 for i in range(RB):
                     for a in range(CB):
@@ -223,9 +226,7 @@ def tile_bdhhrm_b_kernel(tc, table, h_init, l_init, enc, enc_v, dec, cos_t, sin_
                             start=(a == 0),
                             stop=(a == CB - 1),
                         )
-                rstd = pair.tile([P, RB], F32, name="rstd_tok")
-                nc.scalar.activation(out=rstd[:], in_=q_ps[:], func=ACT.Abs_reciprocal_sqrt, bias=eps_t[:, 0:1])
-                return rstd
+                nc.scalar.activation(out=rstd_tok[b][:], in_=q_ps[:], func=ACT.Abs_reciprocal_sqrt, bias=eps_t[:, 0:1])
 
             looked_up = [look_up(b) for b in range(B)]
             for b in range(B):
@@ -234,12 +235,12 @@ def tile_bdhhrm_b_kernel(tc, table, h_init, l_init, enc, enc_v, dec, cos_t, sin_
                 rstd = column_rstd(sq)
                 keep_codes(b, 0, x_ps, rstd)
                 keep_codes(b, 4, code_sums(b, 4), rstd)
-                rstd_tok = token_rstd(sq)
+                token_rstd(b, sq)
                 for i in range(RB):
-                    t_ps = bank()
+                    t_ps = bank(dtype=BF16)
                     for a in range(CB):
-                        nc.tensor.transpose(t_ps[:, a * P : (a + 1) * P], u_c[:, a, i * P : (i + 1) * P], ident32[:])
-                    nc.scalar.activation(out=xi_t[b * RB + i][:], in_=t_ps[:], func=ACT.Identity, scale=rstd_tok[:, i : i + 1])
+                        nc.tensor.transpose(t_ps[:, a * P : (a + 1) * P], u16[a][:, b * T + i * P : b * T + (i + 1) * P], ident16[:])
+                    nc.scalar.copy(out=u_t[b * RB + i][:], in_=t_ps[:])
 
             neg_mean = held.tile([P, KB], F32, name="neg_mean")
             for h in range(NH):
@@ -278,9 +279,12 @@ def tile_bdhhrm_b_kernel(tc, table, h_init, l_init, enc, enc_v, dec, cos_t, sin_
                             start=(e == 0),
                             stop=(e == 1),
                         )
-                    nc.vector.tensor_tensor(out=a_t[:, i, lo : lo + P], in0=s_ps[:, lo : lo + P], in1=later[:], op=ALU.mult)
+                    factor = rstd_tok[b][:, i : i + 1]
+                    nc.vector.scalar_tensor_tensor(
+                        out=a_t[:, i, lo : lo + P], in0=s_ps[:, lo : lo + P], scalar=factor, in1=later[:], op0=ALU.mult, op1=ALU.mult
+                    )
                     if lo + P < T:
-                        nc.scalar.copy(out=a_t[:, i, lo + P : T], in_=s_ps[:, lo + P : T])
+                        nc.scalar.activation(out=a_t[:, i, lo + P : T], in_=s_ps[:, lo + P : T], func=ACT.Identity, scale=factor)
                 return a_t
 
             def values(b, a_t):
@@ -291,13 +295,13 @@ def tile_bdhhrm_b_kernel(tc, table, h_init, l_init, enc, enc_v, dec, cos_t, sin_
                     for i in range(RB):
                         nc.tensor.matmul(
                             av_ps[:, i * P : T],
-                            lhsT=xi_t[b * RB + i][:, a * P : (a + 1) * P],
+                            lhsT=u_t[b * RB + i][:, a * P : (a + 1) * P],
                             rhs=a_t[:, i, i * P : T],
                             start=(i == 0),
                             stop=(i == RB - 1),
                         )
                     nc.scalar.copy(out=av[:, a, :], in_=av_ps[:])
-                    nc.scalar.activation(out=sq[:, a, :], in_=av_ps[:], func=ACT.Square)
+                nc.scalar.activation(out=sq[:], in_=av[:], func=ACT.Square)
                 halves = pair.tile([P, 2, W], BF16, name="halves")
                 nc.vector.tensor_tensor(out=halves[:], in0=sq[:, 0:2, :], in1=sq[:, 2:4, :], op=ALU.add)
                 whole = pair.tile([P, 1, W], BF16, name="whole")

@@ -33,7 +33,6 @@ def tile_bdhhrm_b_kernel(tc, table, h_init, l_init, enc, enc_v, dec, cos_t, sin_
             return psum.tile(list(shape), dtype, name="bank", tag="bank")
 
         offsets = held.tile([P, N // 16], U16, name="offsets")
-        nc.sync.dma_start(offsets[:], offs)
 
         mean_w32 = held.tile([P, P], F32, name="mean_w32")
         nc.vector.memset(mean_w32[:], 1.0 / C)
@@ -50,6 +49,14 @@ def tile_bdhhrm_b_kernel(tc, table, h_init, l_init, enc, enc_v, dec, cos_t, sin_
         nc.gpsimd.affine_select(
             out=later[:], in_=later[:], pattern=[[1, P]], compare_op=ALU.is_gt, fill=0.0, base=0, channel_multiplier=-1
         )
+
+        def add_blocks(sq):
+            width = sq.shape[2]
+            halves = pair.tile([P, 2, width], BF16, name="halves", tag=f"halves{width}")
+            nc.vector.tensor_tensor(out=halves[:], in0=sq[:, 0:2, :], in1=sq[:, 2:4, :], op=ALU.add)
+            whole = pair.tile([P, 1, width], BF16, name="whole", tag=f"whole{width}")
+            nc.vector.tensor_tensor(out=whole[:, 0, :], in0=halves[:, 0, :], in1=halves[:, 1, :], op=ALU.add)
+            return whole
 
         def column_rstd(squares):
             blocks, width = squares.shape[1], squares.shape[2]
@@ -121,6 +128,7 @@ def tile_bdhhrm_b_kernel(tc, table, h_init, l_init, enc, enc_v, dec, cos_t, sin_
                 raw.append(piece_tile())
                 for a in range(CB):
                     nc.sync.dma_start(raw[s][:, a, :], table[a * P : (a + 1) * P, s * W : (s + 1) * W])
+            nc.sync.dma_start(offsets[:], offs)
             nc.sync.dma_start(enc_sb[:], enc.rearrange("(a p) k -> p a k", p=P))
             nc.sync.dma_start(ev_sb[:], enc_v.rearrange("(a p) k -> p a k", p=P))
 
@@ -215,27 +223,25 @@ def tile_bdhhrm_b_kernel(tc, table, h_init, l_init, enc, enc_v, dec, cos_t, sin_
                     nc.scalar.activation(out=sq[:, a, :], in_=u_c[:, a, :], func=ACT.Square)
                 return u_c, sq
 
-            def token_rstd(b, sq):
+            def token_rstd(b, whole):
                 q_ps = psum.tile([P, RB], F32, name="q_ps", tag="sums", bufs=1)
                 for i in range(RB):
-                    for a in range(CB):
-                        nc.tensor.matmul(
-                            q_ps[:, i : i + 1],
-                            lhsT=sq[:, a, i * P : (i + 1) * P],
-                            rhs=mean_w16[:, 0:1],
-                            start=(a == 0),
-                            stop=(a == CB - 1),
-                        )
+                    nc.tensor.matmul(
+                        q_ps[:, i : i + 1], lhsT=whole[:, 0, i * P : (i + 1) * P], rhs=mean_w16[:, 0:1], start=True, stop=True
+                    )
                 nc.scalar.activation(out=rstd_tok[b][:], in_=q_ps[:], func=ACT.Abs_reciprocal_sqrt, bias=eps_t[:, 0:1])
 
-            looked_up = [look_up(b) for b in range(B)]
+            looked_up = [look_up(0)]
             for b in range(B):
                 u_c, sq = looked_up[b]
                 x_ps = code_sums(b, 0)
-                rstd = column_rstd(sq)
+                whole = add_blocks(sq)
+                rstd = column_rstd(sq if b == 0 else whole)
+                if b + 1 < B:
+                    looked_up.append(look_up(b + 1))
                 keep_codes(b, 0, x_ps, rstd)
                 keep_codes(b, 4, code_sums(b, 4), rstd)
-                token_rstd(b, sq)
+                token_rstd(b, whole)
                 for i in range(RB):
                     t_ps = bank(dtype=BF16)
                     for a in range(CB):
@@ -302,11 +308,7 @@ def tile_bdhhrm_b_kernel(tc, table, h_init, l_init, enc, enc_v, dec, cos_t, sin_
                         )
                     nc.scalar.copy(out=av[:, a, :], in_=av_ps[:])
                 nc.scalar.activation(out=sq[:], in_=av[:], func=ACT.Square)
-                halves = pair.tile([P, 2, W], BF16, name="halves")
-                nc.vector.tensor_tensor(out=halves[:], in0=sq[:, 0:2, :], in1=sq[:, 2:4, :], op=ALU.add)
-                whole = pair.tile([P, 1, W], BF16, name="whole")
-                nc.vector.tensor_tensor(out=whole[:, 0, :], in0=halves[:, 0, :], in1=halves[:, 1, :], op=ALU.add)
-                return av, whole
+                return av, add_blocks(sq)
 
             def gate(b, h, av, squares):
                 tok = slice(b * T, (b + 1) * T)
@@ -326,6 +328,7 @@ def tile_bdhhrm_b_kernel(tc, table, h_init, l_init, enc, enc_v, dec, cos_t, sin_
 
             def project(b):
                 tok = slice(b * T, (b + 1) * T)
+                last = b == B - 1
                 w_ps = [bank() for a in range(CB)]
                 for blocks in (range(0, KB - 2), range(KB - 2, KB)):
                     for a in range(CB):
@@ -345,7 +348,7 @@ def tile_bdhhrm_b_kernel(tc, table, h_init, l_init, enc, enc_v, dec, cos_t, sin_
                         nc.scalar.activation(out=sq[:, a, :], in_=w_ps[a][:, half], func=ACT.Square)
                     squares.append(sq)
                 for half, sq_w in zip(HALVES, squares):
-                    rstd = column_rstd(sq_w)
+                    rstd = column_rstd(sq_w if last else add_blocks(sq_w))
                     sq = ring.tile([P, CB, T // 2], BF16, name="sq_half")
                     for a in range(CB):
                         nc.vector.tensor_tensor(out=y[:, a, half], in0=w_ps[a][:, half], in1=rstd[:], op=ALU.mult)
@@ -354,15 +357,15 @@ def tile_bdhhrm_b_kernel(tc, table, h_init, l_init, enc, enc_v, dec, cos_t, sin_
                 return y, squares[2:]
 
             def finish(b, y, squares):
+                last = b == B - 1
                 res = back.tile([P, CB, T], F32, name="res")
                 for half, sq in zip(HALVES, squares):
-                    rstd = column_rstd(sq)
+                    rstd = column_rstd(sq if last else add_blocks(sq))
                     for a in range(CB):
                         nc.vector.scalar_tensor_tensor(
                             out=res[:, a, half], in0=y[:, a, half], scalar=l_c[:, a : a + 1], in1=rstd[:], op0=ALU.add, op1=ALU.mult
                         )
-                for a in range(CB):
-                    nc.sync.dma_start(out[a * P : (a + 1) * P, b * T : (b + 1) * T], res[:, a, :])
+                        nc.sync.dma_start(out[a * P : (a + 1) * P, b * T + half.start : b * T + half.stop], res[:, a, half])
 
             heads = [(b, h) for b in range(B) for h in range(NH)]
             count = len(heads)

@@ -78,8 +78,7 @@ def tile_bdhhrm_b_kernel(tc, table, h_init, l_init, enc, enc_v, dec, cos_t, sin_
         rstd_tok = [held.tile([P, RB], F32, name=f"rstd_tok{b}") for b in range(B)]
         enc_sb = held.tile([P, CB, HN], BF16, name="enc_sb")
         ev_sb = held.tile([P, CB, HN], BF16, name="ev_sb")
-        cos_q = held.tile([P, 2, T], BF16, name="cos_q")
-        sin_x = held.tile([P, 2, T], BF16, name="sin_x")
+        turn = held.tile([P, 2, 2, T], BF16, name="turn")
 
         xs = held.tile([P, KB, N], BF16, name="xs")
         qr = held.tile([P, KB, N], BF16, name="qr")
@@ -110,12 +109,10 @@ def tile_bdhhrm_b_kernel(tc, table, h_init, l_init, enc, enc_v, dec, cos_t, sin_
 
         def rotate(b, h):
             tok = slice(b * T, (b + 1) * T)
-            own = pair.tile([P, 2, T], BF16, name="own")
-            other = pair.tile([P, 2, T], BF16, name="other")
-            nc.vector.tensor_tensor(out=own[:], in0=xs[:, 2 * h : 2 * h + 2, tok], in1=cos_q[:], op=ALU.mult)
-            nc.vector.tensor_tensor(out=other[:], in0=xs[:, 2 * h : 2 * h + 2, tok], in1=sin_x[:], op=ALU.mult)
-            for e in range(2):
-                nc.vector.tensor_tensor(out=qr[:, 2 * h + e, tok], in0=own[:, e, :], in1=other[:, 1 - e, :], op=ALU.add)
+            rows = xs[:, 2 * h : 2 * h + 2, tok]
+            parts = pair.tile([P, 2, 2, T], BF16, name="parts")
+            nc.vector.tensor_tensor(out=parts[:], in0=rows.unsqueeze(1).to_broadcast([P, 2, 2, T]), in1=turn[:], op=ALU.mult)
+            nc.vector.tensor_tensor(out=qr[:, 2 * h : 2 * h + 2, tok], in0=parts[:, 0], in1=parts[:, 1, ::-1, :], op=ALU.add)
 
         with tc.tile_pool(name="front", bufs=1) as front:
 
@@ -203,10 +200,10 @@ def tile_bdhhrm_b_kernel(tc, table, h_init, l_init, enc, enc_v, dec, cos_t, sin_
             nc.sync.dma_start(rotary[:, 0:2, :], cos_t.rearrange("(p e) t -> p e t", e=2))
             nc.sync.dma_start(rotary[:, 2:4, :], sin_t.rearrange("(p e) t -> p e t", e=2))
 
-            nc.gpsimd.tensor_scalar(out=cos_q[:], in0=rotary[:, 0:2, :], scalar1=0.25, scalar2=0.0, op0=ALU.mult, op1=ALU.add)
+            nc.gpsimd.tensor_scalar(out=turn[:, 0], in0=rotary[:, 0:2, :], scalar1=0.25, scalar2=0.0, op0=ALU.mult, op1=ALU.add)
             for e in range(2):
                 nc.gpsimd.tensor_scalar(
-                    out=sin_x[:, e, :], in0=rotary[:, 3 - e, :], scalar1=0.25, scalar2=0.0, op0=ALU.mult, op1=ALU.add
+                    out=turn[:, 1, e, :], in0=rotary[:, 3 - e, :], scalar1=0.25, scalar2=0.0, op0=ALU.mult, op1=ALU.add
                 )
 
             def look_up(b):
@@ -323,8 +320,12 @@ def tile_bdhhrm_b_kernel(tc, table, h_init, l_init, enc, enc_v, dec, cos_t, sin_
                         out=prod[:, e, :], in0=v_ps[:], scalar=0.0, in1=xs[:, 2 * h + e, tok], op0=ALU.max, op1=ALU.mult
                     )
                 rstd = column_rstd(squares)
-                for e in range(2):
-                    nc.vector.tensor_tensor(out=gated[:, 2 * h + e, tok], in0=prod[:, e, :], in1=rstd[:], op=ALU.mult)
+                nc.vector.tensor_tensor(
+                    out=gated[:, 2 * h : 2 * h + 2, tok], in0=prod[:], in1=rstd[:].unsqueeze(1).to_broadcast([P, 2, T]), op=ALU.mult
+                )
+
+            def parts_of(b):
+                return HALVES if b == B - 1 else (slice(0, T),)
 
             def project(b):
                 tok = slice(b * T, (b + 1) * T)
@@ -341,31 +342,32 @@ def tile_bdhhrm_b_kernel(tc, table, h_init, l_init, enc, enc_v, dec, cos_t, sin_
                                 stop=(k == KB - 1),
                             )
                 y = back.tile([P, CB, T], F32, name="y")
+                squares_w = []
+                for part in parts_of(b):
+                    sq = ring.tile([P, CB, part.stop - part.start], BF16, name="sq")
+                    for a in range(CB):
+                        nc.scalar.activation(out=sq[:, a, :], in_=w_ps[a][:, part], func=ACT.Square)
+                    squares_w.append(sq)
                 squares = []
-                for half in HALVES:
-                    sq = ring.tile([P, CB, T // 2], BF16, name="sq_half")
-                    for a in range(CB):
-                        nc.scalar.activation(out=sq[:, a, :], in_=w_ps[a][:, half], func=ACT.Square)
-                    squares.append(sq)
-                for half, sq_w in zip(HALVES, squares):
+                for part, sq_w in zip(parts_of(b), squares_w):
                     rstd = column_rstd(sq_w if last else add_blocks(sq_w))
-                    sq = ring.tile([P, CB, T // 2], BF16, name="sq_half")
+                    sq = ring.tile([P, CB, part.stop - part.start], BF16, name="sq")
                     for a in range(CB):
-                        nc.vector.tensor_tensor(out=y[:, a, half], in0=w_ps[a][:, half], in1=rstd[:], op=ALU.mult)
-                        nc.scalar.activation(out=sq[:, a, :], in_=y[:, a, half], func=ACT.Square, bias=l_c[:, a : a + 1])
+                        nc.vector.tensor_tensor(out=y[:, a, part], in0=w_ps[a][:, part], in1=rstd[:], op=ALU.mult)
+                        nc.scalar.activation(out=sq[:, a, :], in_=y[:, a, part], func=ACT.Square, bias=l_c[:, a : a + 1])
                     squares.append(sq)
-                return y, squares[2:]
+                return y, squares
 
             def finish(b, y, squares):
                 last = b == B - 1
                 res = back.tile([P, CB, T], F32, name="res")
-                for half, sq in zip(HALVES, squares):
+                for part, sq in zip(parts_of(b), squares):
                     rstd = column_rstd(sq if last else add_blocks(sq))
                     for a in range(CB):
                         nc.vector.scalar_tensor_tensor(
-                            out=res[:, a, half], in0=y[:, a, half], scalar=l_c[:, a : a + 1], in1=rstd[:], op0=ALU.add, op1=ALU.mult
+                            out=res[:, a, part], in0=y[:, a, part], scalar=l_c[:, a : a + 1], in1=rstd[:], op0=ALU.add, op1=ALU.mult
                         )
-                        nc.sync.dma_start(out[a * P : (a + 1) * P, b * T + half.start : b * T + half.stop], res[:, a, half])
+                        nc.sync.dma_start(out[a * P : (a + 1) * P, b * T + part.start : b * T + part.stop], res[:, a, part])
 
             heads = [(b, h) for b in range(B) for h in range(NH)]
             count = len(heads)

@@ -164,18 +164,28 @@ def tile_bdhhrm_b_kernel(tc, table, h_init, l_init, enc, enc_v, dec, cos_t, sin_
                     nc.vector.bn_stats(out=stats[:], in_=f_ps[:])
                     mean_var = ring.tile([P, 2], F32, name="mean_var")
                     nc.vector.bn_aggr(out=mean_var[:], in_=stats[:])
-                    neg_m = ring.tile([P, 1], F32, name="neg_m")
-                    nc.vector.tensor_scalar(out=neg_m[:], in0=mean_var[:, 0:1], scalar1=-1.0, scalar2=None, op0=ALU.mult)
                     factor = ring.tile([P, 1], F32, name="factor")
                     nc.scalar.activation(
                         out=factor[:], in_=mean_var[:, 1:2], func=ACT.Abs_reciprocal_sqrt, bias=eps_t[:, 0:1]
                     )
-                    shift = ring.tile([P, 1], F32, name="shift")
-                    nc.scalar.activation(out=shift[:], in_=factor[:], func=ACT.Identity, scale=neg_m[:, 0:1])
                     words = front.tile([P, C], F32, name="words", bufs=2 * groups)
-                    nc.scalar.activation(
-                        out=words[:], in_=f_ps[:], func=ACT.Identity, scale=factor[:, 0:1], bias=shift[:, 0:1]
-                    )
+                    if g % 2 == 1:
+                        nc.vector.tensor_scalar(
+                            out=words[:],
+                            in0=f_ps[:],
+                            scalar1=mean_var[:, 0:1],
+                            scalar2=factor[:, 0:1],
+                            op0=ALU.subtract,
+                            op1=ALU.mult,
+                        )
+                    else:
+                        neg_m = ring.tile([P, 1], F32, name="neg_m")
+                        nc.vector.tensor_scalar(out=neg_m[:], in0=mean_var[:, 0:1], scalar1=-1.0, scalar2=None, op0=ALU.mult)
+                        shift = ring.tile([P, 1], F32, name="shift")
+                        nc.scalar.activation(out=shift[:], in_=factor[:], func=ACT.Identity, scale=neg_m[:, 0:1])
+                        nc.scalar.activation(
+                            out=words[:], in_=f_ps[:], func=ACT.Identity, scale=factor[:, 0:1], bias=shift[:, 0:1]
+                        )
                     flipped.append(words)
                 return flipped
 
@@ -184,7 +194,7 @@ def tile_bdhhrm_b_kernel(tc, table, h_init, l_init, enc, enc_v, dec, cos_t, sin_
                     b_ps = bank()
                     for g in range(groups):
                         nc.tensor.transpose(b_ps[:, g * P : (g + 1) * P], flipped[g][:, a * P : (a + 1) * P], ident32[:])
-                    if a % 2 == 0:
+                    if s == pieces - 1 and a == 0:
                         nc.vector.tensor_copy(tn[a][:, s * W : (s + 1) * W], b_ps[:])
                     else:
                         nc.scalar.copy(out=tn[a][:, s * W : (s + 1) * W], in_=b_ps[:])

@@ -123,33 +123,17 @@ def tile_bdhhrm_b_kernel(tc, table, h_init, l_init, enc, enc_v, dec, cos_t, sin_
             raw = []
             for s in range(pieces):
                 raw.append(piece_tile())
-                for a in range(CB):
-                    nc.sync.dma_start(raw[s][:, a, :], table[a * P : (a + 1) * P, s * W : (s + 1) * W])
+                if s == 0:
+                    for g in range(W // P):
+                        nc.sync.dma_start(
+                            raw[s][:, :, g * P : (g + 1) * P], table.rearrange("(a p) s -> p a s", p=P)[:, :, g * P : (g + 1) * P]
+                        )
+                else:
+                    for a in range(CB):
+                        nc.sync.dma_start(raw[s][:, a, :], table[a * P : (a + 1) * P, s * W : (s + 1) * W])
             nc.sync.dma_start(offsets[:], offs)
             nc.sync.dma_start(enc_sb[:], enc.rearrange("(a p) k -> p a k", p=P))
             nc.sync.dma_start(ev_sb[:], enc_v.rearrange("(a p) k -> p a k", p=P))
-
-            both = held.tile([P, 2 * CB], F32, name="both")
-            nc.vector.tensor_tensor(out=both[:, 0:CB], in0=h_t[:], in1=l_t[:], op=ALU.add)
-            nc.vector.tensor_copy(both[:, CB : 2 * CB], l_t[:])
-            part_ps = bank((P, 2 * CB))
-            nc.tensor.matmul(part_ps[:], lhsT=mean_w32[:], rhs=both[:], start=True, stop=True)
-            means = held.tile([P, 2], F32, name="means")
-            centred = held.tile([P, 2 * CB], F32, name="centred")
-            for v in range(2):
-                nc.vector.reduce_sum(out=means[:, v : v + 1], in_=part_ps[:, v * CB : (v + 1) * CB], axis=AX.X)
-                nc.vector.tensor_scalar(
-                    out=centred[:, v * CB : (v + 1) * CB],
-                    in0=both[:, v * CB : (v + 1) * CB],
-                    scalar1=means[:, v : v + 1],
-                    scalar2=None,
-                    op0=ALU.subtract,
-                )
-            z0_c = centred[:, 0:CB]
-            l_c = centred[:, CB : 2 * CB]
-            z0_wide = [front.tile([P, W], F32, name=f"z0_wide{a}") for a in range(CB)]
-            for a in range(CB):
-                nc.vector.tensor_copy(z0_wide[a][:], z0_c[:, a : a + 1].to_broadcast([P, W]))
 
             tn = [front.tile([P, S], F32, name=f"tn{a}") for a in range(CB)]
             groups = W // P
@@ -200,6 +184,29 @@ def tile_bdhhrm_b_kernel(tc, table, h_init, l_init, enc, enc_v, dec, cos_t, sin_
                         nc.scalar.copy(out=tn[a][:, s * W : (s + 1) * W], in_=b_ps[:])
 
             flipped_next = normalise(0)
+
+            both = held.tile([P, 2 * CB], F32, name="both")
+            nc.vector.tensor_tensor(out=both[:, 0:CB], in0=h_t[:], in1=l_t[:], op=ALU.add)
+            nc.vector.tensor_copy(both[:, CB : 2 * CB], l_t[:])
+            part_ps = bank((P, 2 * CB))
+            nc.tensor.matmul(part_ps[:], lhsT=mean_w32[:], rhs=both[:], start=True, stop=True)
+            means = held.tile([P, 2], F32, name="means")
+            centred = held.tile([P, 2 * CB], F32, name="centred")
+            for v in range(2):
+                nc.vector.reduce_sum(out=means[:, v : v + 1], in_=part_ps[:, v * CB : (v + 1) * CB], axis=AX.X)
+                nc.vector.tensor_scalar(
+                    out=centred[:, v * CB : (v + 1) * CB],
+                    in0=both[:, v * CB : (v + 1) * CB],
+                    scalar1=means[:, v : v + 1],
+                    scalar2=None,
+                    op0=ALU.subtract,
+                )
+            z0_c = centred[:, 0:CB]
+            l_c = centred[:, CB : 2 * CB]
+            z0_wide = [front.tile([P, W], F32, name=f"z0_wide{a}") for a in range(CB)]
+            for a in range(CB):
+                nc.vector.tensor_copy(z0_wide[a][:], z0_c[:, a : a + 1].to_broadcast([P, W]))
+
             for s in range(pieces):
                 flipped_now = flipped_next
                 if s + 1 < pieces:

@@ -58,9 +58,12 @@ def tile_bdhhrm_b_kernel(tc, table, h_init, l_init, enc, enc_v, dec, cos_t, sin_
             nc.vector.tensor_tensor(out=whole[:, 0, :], in0=halves[:, 0, :], in1=halves[:, 1, :], op=ALU.add)
             return whole
 
-        def column_rstd(squares):
+        def column_rstd(squares, any_bank=False):
             blocks, width = squares.shape[1], squares.shape[2]
-            q_ps = psum.tile([P, width], F32, name="q_ps", tag="sums", bufs=1)
+            if any_bank:
+                q_ps = bank((P, width))
+            else:
+                q_ps = psum.tile([P, width], F32, name="q_ps", tag="sums", bufs=1)
             for a in range(blocks):
                 nc.tensor.matmul(q_ps[:], lhsT=mean_w16[:], rhs=squares[:, a, :], start=(a == 0), stop=(a == blocks - 1))
             rstd = ring.tile([P, width], F32, name="rstd")
@@ -367,7 +370,7 @@ def tile_bdhhrm_b_kernel(tc, table, h_init, l_init, enc, enc_v, dec, cos_t, sin_
                     squares_w.append(sq)
                 squares = []
                 for part, sq_w in zip(parts_of(b), squares_w):
-                    rstd = column_rstd(sq_w if last else add_blocks(sq_w))
+                    rstd = column_rstd(sq_w if last else add_blocks(sq_w), any_bank=last)
                     sq = ring.tile([P, CB, part.stop - part.start], BF16, name="sq")
                     for a in range(CB):
                         nc.vector.tensor_tensor(out=y[:, a, part], in0=w_ps[a][:, part], in1=rstd[:], op=ALU.mult)
@@ -379,7 +382,7 @@ def tile_bdhhrm_b_kernel(tc, table, h_init, l_init, enc, enc_v, dec, cos_t, sin_
                 last = b == B - 1
                 res = back.tile([P, CB, T], F32, name="res")
                 for part, sq in zip(parts_of(b), squares):
-                    rstd = column_rstd(sq if last else add_blocks(sq))
+                    rstd = column_rstd(sq if last else add_blocks(sq), any_bank=last)
                     for a in range(CB):
                         nc.vector.scalar_tensor_tensor(
                             out=res[:, a, part], in0=y[:, a, part], scalar=l_c[:, a : a + 1], in1=rstd[:], op0=ALU.add, op1=ALU.mult

@@ -216,16 +216,6 @@ def tile_bdhhrm_b_kernel(tc, table, h_init, l_init, enc, enc_v, dec, cos_t, sin_
                     flipped_next = normalise(s + 1)
                 flip_back(s, flipped_now)
 
-            rotary = piece_tile()
-            nc.sync.dma_start(rotary[:, 0:2, :], cos_t.rearrange("(p e) t -> p e t", e=2))
-            nc.sync.dma_start(rotary[:, 2:4, :], sin_t.rearrange("(p e) t -> p e t", e=2))
-
-            nc.gpsimd.tensor_scalar(out=turn[:, 0], in0=rotary[:, 0:2, :], scalar1=0.25, scalar2=0.0, op0=ALU.mult, op1=ALU.add)
-            for e in range(2):
-                nc.gpsimd.tensor_scalar(
-                    out=turn[:, 1, e, :], in0=rotary[:, 3 - e, :], scalar1=0.25, scalar2=0.0, op0=ALU.mult, op1=ALU.add
-                )
-
             def look_up(b):
                 u_c = piece_tile()
                 sq = ring.tile([P, CB, W], BF16, name="sq")
@@ -265,6 +255,13 @@ def tile_bdhhrm_b_kernel(tc, table, h_init, l_init, enc, enc_v, dec, cos_t, sin_
                         nc.tensor.transpose(t_ps[:, a * P : (a + 1) * P], u16[a][:, b * T + i * P : b * T + (i + 1) * P], ident16[:])
                     nc.scalar.copy(out=u_t[b * RB + i][:], in_=t_ps[:])
 
+            rotary = looked_up[1][0]
+            nc.sync.dma_start(rotary[:, 0:2, :], cos_t.rearrange("(p e) t -> p e t", e=2))
+            nc.sync.dma_start(rotary[:, 2:4, :], sin_t.rearrange("(p e) t -> p e t", e=2))
+            nc.scalar.activation(out=turn[:, 0], in_=rotary[:, 0:2, :], func=ACT.Copy, scale=0.25)
+            for e in range(2):
+                nc.scalar.activation(out=turn[:, 1, e, :], in_=rotary[:, 3 - e, :], func=ACT.Copy, scale=0.25)
+
             neg_mean = held.tile([P, KB], F32, name="neg_mean")
             for h in range(NH):
                 dec_rows = looked_up[0][0][:, h, :].bitcast(BF16)
@@ -279,13 +276,12 @@ def tile_bdhhrm_b_kernel(tc, table, h_init, l_init, enc, enc_v, dec, cos_t, sin_
                         scale=-1.0 / C,
                         accum_out=neg_mean[:, k : k + 1],
                     )
-                    nc.gpsimd.tensor_scalar(
+                    nc.vector.tensor_scalar(
                         out=dec_c[:, k, :],
                         in0=dec_rows[:, e * C : (e + 1) * C],
-                        scalar1=1.0,
-                        scalar2=neg_mean[:, k : k + 1],
-                        op0=ALU.mult,
-                        op1=ALU.add,
+                        scalar1=neg_mean[:, k : k + 1],
+                        scalar2=None,
+                        op0=ALU.add,
                     )
 
         with tc.tile_pool(name="back", bufs=2) as back:

import concourse.mybir as mybir
from concourse.masks import make_identity

F32 = mybir.dt.float32
BF16 = mybir.dt.bfloat16
U16 = mybir.dt.uint16
ALU = mybir.AluOpType
ACT = mybir.ActivationFunctionType
AX = mybir.AxisListType

P = 128
C, S, N, B, T, NH, NS, HN = 512, 2048, 1024, 2, 512, 4, 256, 1024
CB = C // P
KB = HN // P
RB = T // P
W = 512
EPS = 1e-5
HALVES = (slice(0, T // 2), slice(T // 2, T))

FLOPS = 2 * (C * HN * N + B * NH * (NS + C) * (T * (T - 1) // 2) + C * HN * N + HN * C * N)


def tile_bdhhrm_b_kernel(tc, table, h_init, l_init, enc, enc_v, dec, cos_t, sin_t, offs, out):
    nc = tc.nc
    with (
        tc.tile_pool(name="held", bufs=1) as held,
        tc.tile_pool(name="pair", bufs=2) as pair,
        tc.tile_pool(name="ring", bufs=3) as ring,
        tc.psum_pool(name="psum", bufs=7) as psum,
    ):

        def bank(shape=(P, W), dtype=F32):
            return psum.tile(list(shape), dtype, name="bank", tag="bank")

        offsets = held.tile([P, N // 16], U16, name="offsets")

        mean_w32 = held.tile([P, P], F32, name="mean_w32")
        nc.vector.memset(mean_w32[:], 1.0 / C)
        mean_w16 = held.tile([P, P], BF16, name="mean_w16")
        nc.vector.memset(mean_w16[:], 1.0 / C)
        eps_t = held.tile([P, 1], F32, name="eps_t")
        nc.vector.memset(eps_t[:], EPS)
        ident32 = held.tile([P, P], F32, name="ident32")
        make_identity(nc, ident32[:])
        ident16 = held.tile([P, P], BF16, name="ident16")
        make_identity(nc, ident16[:])
        later = held.tile([P, P], F32, name="later")
        nc.gpsimd.memset(later[:], 1.0)
        nc.gpsimd.affine_select(
            out=later[:], in_=later[:], pattern=[[1, P]], compare_op=ALU.is_gt, fill=0.0, base=0, channel_multiplier=-1
        )

        def add_blocks(sq):
            width = sq.shape[2]
            halves = pair.tile([P, 2, width], BF16, name="halves", tag=f"halves{width}")
            nc.vector.tensor_tensor(out=halves[:], in0=sq[:, 0:2, :], in1=sq[:, 2:4, :], op=ALU.add)
            whole = pair.tile([P, 1, width], BF16, name="whole", tag=f"whole{width}")
            nc.vector.tensor_tensor(out=whole[:, 0, :], in0=halves[:, 0, :], in1=halves[:, 1, :], op=ALU.add)
            return whole

        def column_rstd(squares, any_bank=False):
            blocks, width = squares.shape[1], squares.shape[2]
            if any_bank:
                q_ps = bank((P, width))
            else:
                q_ps = psum.tile([P, width], F32, name="q_ps", tag="sums", bufs=1)
            for a in range(blocks):
                nc.tensor.matmul(q_ps[:], lhsT=mean_w16[:], rhs=squares[:, a, :], start=(a == 0), stop=(a == blocks - 1))
            rstd = ring.tile([P, width], F32, name="rstd")
            nc.scalar.activation(out=rstd[:], in_=q_ps[:], func=ACT.Abs_reciprocal_sqrt, bias=eps_t[:, 0:1])
            return rstd

        h_t = held.tile([P, CB], F32, name="h_t")
        l_t = held.tile([P, CB], F32, name="l_t")
        with nc.allow_non_contiguous_dma(reason="512 values, one to a partition and block"):
            nc.scalar.dma_start(h_t[:], h_init.rearrange("(a p) o -> p (a o)", p=P))
            nc.scalar.dma_start(l_t[:], l_init.rearrange("(a p) o -> p (a o)", p=P))

        u16 = [held.tile([P, N], BF16, name=f"u16_{a}") for a in range(CB)]
        u_t = [held.tile([P, C], BF16, name=f"u_t{j}") for j in range(N // P)]
        rstd_tok = [held.tile([P, RB], F32, name=f"rstd_tok{b}") for b in range(B)]
        enc_sb = held.tile([P, CB, HN], BF16, name="enc_sb")
        ev_sb = held.tile([P, CB, HN], BF16, name="ev_sb")
        turn = held.tile([P, 2, 2, T], BF16, name="turn")

        xs = held.tile([P, KB, N], BF16, name="xs")
        qr = held.tile([P, KB, N], BF16, name="qr")
        gated = held.tile([P, KB, N], BF16, name="gated")
        dec_c = held.tile([P, KB, C], BF16, name="dec_c")

        def rows_of(h, e):
            return slice(h * NS + e, (h + 1) * NS, 2)

        def code_sums(b, k0):
            x_ps = [bank() for k in range(4)]
            for a in range(CB):
                for k in range(4):
                    nc.tensor.matmul(
                        x_ps[k][:],
                        lhsT=enc_sb[:, a, rows_of((k0 + k) // 2, k % 2)],
                        rhs=u16[a][:, b * T : (b + 1) * T],
                        start=(a == 0),
                        stop=(a == CB - 1),
                    )
            return x_ps

        def keep_codes(b, k0, x_ps, rstd):
            for k in range(4):
                nc.vector.scalar_tensor_tensor(
                    out=xs[:, k0 + k, b * T : (b + 1) * T], in0=x_ps[k][:], scalar=0.0, in1=rstd[:], op0=ALU.max, op1=ALU.mult
                )

        def rotate(b, h):
            tok = slice(b * T, (b + 1) * T)
            rows = xs[:, 2 * h : 2 * h + 2, tok]
            parts = pair.tile([P, 2, 2, T], BF16, name="parts")
            nc.vector.tensor_tensor(out=parts[:], in0=rows.unsqueeze(1).to_broadcast([P, 2, 2, T]), in1=turn[:], op=ALU.mult)
            nc.vector.tensor_tensor(out=qr[:, 2 * h : 2 * h + 2, tok], in0=parts[:, 0], in1=parts[:, 1, ::-1, :], op=ALU.add)

        with tc.tile_pool(name="front", bufs=1) as front:

            def piece_tile():
                return front.tile([P, CB, W], F32, name="piece", tag="piece", bufs=4)

            pieces = S // W
            raw = []
            for s in range(pieces):
                raw.append(piece_tile())
                if s == 0:
                    for g in range(W // P):
                        nc.sync.dma_start(
                            raw[s][:, :, g * P : (g + 1) * P], table.rearrange("(a p) s -> p a s", p=P)[:, :, g * P : (g + 1) * P]
                        )
                else:
                    for a in range(CB):
                        nc.sync.dma_start(raw[s][:, a, :], table[a * P : (a + 1) * P, s * W : (s + 1) * W])
            nc.sync.dma_start(offsets[:], offs)
            nc.sync.dma_start(enc_sb[:], enc.rearrange("(a p) k -> p a k", p=P))
            nc.sync.dma_start(ev_sb[:], enc_v.rearrange("(a p) k -> p a k", p=P))

            tn = [front.tile([P, S], F32, name=f"tn{a}") for a in range(CB)]
            groups = W // P

            def normalise(s):
                flipped = []
                for g in range(groups):
                    f_ps = bank()
                    for a in range(CB):
                        nc.tensor.transpose(f_ps[:, a * P : (a + 1) * P], raw[s][:, a, g * P : (g + 1) * P], ident32[:])
                    stats = ring.tile([P, 6], F32, name="stats")
                    nc.vector.bn_stats(out=stats[:], in_=f_ps[:])
                    mean_var = ring.tile([P, 2], F32, name="mean_var")
                    nc.vector.bn_aggr(out=mean_var[:], in_=stats[:])
                    factor = ring.tile([P, 1], F32, name="factor")
                    nc.scalar.activation(
                        out=factor[:], in_=mean_var[:, 1:2], func=ACT.Abs_reciprocal_sqrt, bias=eps_t[:, 0:1]
                    )
                    words = front.tile([P, C], F32, name="words", bufs=2 * groups)
                    if g % 2 == 1:
                        nc.vector.tensor_scalar(
                            out=words[:],
                            in0=f_ps[:],
                            scalar1=mean_var[:, 0:1],
                            scalar2=factor[:, 0:1],
                            op0=ALU.subtract,
                            op1=ALU.mult,
                        )
                    else:
                        neg_m = ring.tile([P, 1], F32, name="neg_m")
                        nc.vector.tensor_scalar(out=neg_m[:], in0=mean_var[:, 0:1], scalar1=-1.0, scalar2=None, op0=ALU.mult)
                        shift = ring.tile([P, 1], F32, name="shift")
                        nc.scalar.activation(out=shift[:], in_=factor[:], func=ACT.Identity, scale=neg_m[:, 0:1])
                        nc.scalar.activation(
                            out=words[:], in_=f_ps[:], func=ACT.Identity, scale=factor[:, 0:1], bias=shift[:, 0:1]
                        )
                    flipped.append(words)
                return flipped

            def flip_back(s, flipped):
                for a in range(CB):
                    b_ps = bank()
                    for g in range(groups):
                        nc.tensor.transpose(b_ps[:, g * P : (g + 1) * P], flipped[g][:, a * P : (a + 1) * P], ident32[:])
                    if s == pieces - 1 and a == 0:
                        nc.vector.tensor_copy(tn[a][:, s * W : (s + 1) * W], b_ps[:])
                    else:
                        nc.scalar.copy(out=tn[a][:, s * W : (s + 1) * W], in_=b_ps[:])

            flipped_next = normalise(0)

            both = held.tile([P, 2 * CB], F32, name="both")
            nc.vector.tensor_tensor(out=both[:, 0:CB], in0=h_t[:], in1=l_t[:], op=ALU.add)
            nc.vector.tensor_copy(both[:, CB : 2 * CB], l_t[:])
            part_ps = bank((P, 2 * CB))
            nc.tensor.matmul(part_ps[:], lhsT=mean_w32[:], rhs=both[:], start=True, stop=True)
            means = held.tile([P, 2], F32, name="means")
            centred = held.tile([P, 2 * CB], F32, name="centred")
            for v in range(2):
                nc.vector.reduce_sum(out=means[:, v : v + 1], in_=part_ps[:, v * CB : (v + 1) * CB], axis=AX.X)
                nc.vector.tensor_scalar(
                    out=centred[:, v * CB : (v + 1) * CB],
                    in0=both[:, v * CB : (v + 1) * CB],
                    scalar1=means[:, v : v + 1],
                    scalar2=None,
                    op0=ALU.subtract,
                )
            z0_c = centred[:, 0:CB]
            l_c = centred[:, CB : 2 * CB]
            z0_wide = [front.tile([P, W], F32, name=f"z0_wide{a}") for a in range(CB)]
            for a in range(CB):
                nc.vector.tensor_copy(z0_wide[a][:], z0_c[:, a : a + 1].to_broadcast([P, W]))

            for s in range(pieces):
                flipped_now = flipped_next
                if s + 1 < pieces:
                    flipped_next = normalise(s + 1)
                flip_back(s, flipped_now)

            def look_up(b):
                u_c = piece_tile()
                sq = ring.tile([P, CB, W], BF16, name="sq")
                for a in range(CB):
                    nc.vector.tensor_tensor(
                        out=u_c[:, a, :],
                        in0=tn[a][:].indirect(offsets[:, b * (T // 16) : (b + 1) * (T // 16)]),
                        in1=z0_wide[a][:],
                        op=ALU.add,
                    )
                    nc.scalar.copy(out=u16[a][:, b * T : (b + 1) * T], in_=u_c[:, a, :])
                    nc.scalar.activation(out=sq[:, a, :], in_=u_c[:, a, :], func=ACT.Square)
                return u_c, sq

            def token_rstd(b, whole):
                q_ps = psum.tile([P, RB], F32, name="q_ps", tag="sums", bufs=1)
                for i in range(RB):
                    nc.tensor.matmul(
                        q_ps[:, i : i + 1], lhsT=whole[:, 0, i * P : (i + 1) * P], rhs=mean_w16[:, 0:1], start=True, stop=True
                    )
                nc.scalar.activation(out=rstd_tok[b][:], in_=q_ps[:], func=ACT.Abs_reciprocal_sqrt, bias=eps_t[:, 0:1])

            looked_up = [look_up(0)]
            for b in range(B):
                u_c, sq = looked_up[b]
                x_ps = code_sums(b, 0)
                whole = add_blocks(sq)
                rstd = column_rstd(sq if b == 0 else whole)
                if b + 1 < B:
                    looked_up.append(look_up(b + 1))
                keep_codes(b, 0, x_ps, rstd)
                keep_codes(b, 4, code_sums(b, 4), rstd)
                token_rstd(b, whole)
                for i in range(RB):
                    t_ps = bank(dtype=BF16)
                    for a in range(CB):
                        nc.tensor.transpose(t_ps[:, a * P : (a + 1) * P], u16[a][:, b * T + i * P : b * T + (i + 1) * P], ident16[:])
                    nc.scalar.copy(out=u_t[b * RB + i][:], in_=t_ps[:])

            rotary = looked_up[1][0]
            nc.sync.dma_start(rotary[:, 0:2, :], cos_t.rearrange("(p e) t -> p e t", e=2))
            nc.sync.dma_start(rotary[:, 2:4, :], sin_t.rearrange("(p e) t -> p e t", e=2))
            nc.scalar.activation(out=turn[:, 0], in_=rotary[:, 0:2, :], func=ACT.Copy, scale=0.25)
            for e in range(2):
                nc.scalar.activation(out=turn[:, 1, e, :], in_=rotary[:, 3 - e, :], func=ACT.Copy, scale=0.25)

            neg_mean = held.tile([P, KB], F32, name="neg_mean")
            for h in range(NH):
                dec_rows = looked_up[0][0][:, h, :].bitcast(BF16)
                nc.sync.dma_start(dec_rows, dec[h * NS : (h + 1) * NS, :].rearrange("(p e) c -> p (e c)", e=2))
                for e in range(2):
                    k = 2 * h + e
                    unused = pair.tile([P, C], BF16, name="unused")
                    nc.scalar.activation(
                        out=unused[:],
                        in_=dec_rows[:, e * C : (e + 1) * C],
                        func=ACT.Copy,
                        scale=-1.0 / C,
                        accum_out=neg_mean[:, k : k + 1],
                    )
                    nc.vector.tensor_scalar(
                        out=dec_c[:, k, :],
                        in0=dec_rows[:, e * C : (e + 1) * C],
                        scalar1=neg_mean[:, k : k + 1],
                        scalar2=None,
                        op0=ALU.add,
                    )

        with tc.tile_pool(name="back", bufs=2) as back:
            def scores(b, h):
                a_t = back.tile([P, RB, T], BF16, name="a_t")
                for i in range(RB):
                    lo = i * P
                    s_ps = bank()
                    for e in range(2):
                        nc.tensor.matmul(
                            s_ps[:, lo:T],
                            lhsT=qr[:, 2 * h + e, b * T + lo : b * T + lo + P],
                            rhs=qr[:, 2 * h + e, b * T + lo : (b + 1) * T],
                            start=(e == 0),
                            stop=(e == 1),
                        )
                    factor = rstd_tok[b][:, i : i + 1]
                    nc.vector.scalar_tensor_tensor(
                        out=a_t[:, i, lo : lo + P], in0=s_ps[:, lo : lo + P], scalar=factor, in1=later[:], op0=ALU.mult, op1=ALU.mult
                    )
                    if lo + P < T:
                        nc.scalar.activation(out=a_t[:, i, lo + P : T], in_=s_ps[:, lo + P : T], func=ACT.Identity, scale=factor)
                return a_t

            def values(b, a_t):
                av = back.tile([P, CB, T], BF16, name="av")
                sq = ring.tile([P, CB, W], BF16, name="sq")
                for a in range(CB):
                    av_ps = bank()
                    for i in range(RB):
                        nc.tensor.matmul(
                            av_ps[:, i * P : T],
                            lhsT=u_t[b * RB + i][:, a * P : (a + 1) * P],
                            rhs=a_t[:, i, i * P : T],
                            start=(i == 0),
                            stop=(i == RB - 1),
                        )
                    nc.scalar.copy(out=av[:, a, :], in_=av_ps[:])
                nc.scalar.activation(out=sq[:], in_=av[:], func=ACT.Square)
                return av, add_blocks(sq)

            def gate(b, h, av, squares):
                tok = slice(b * T, (b + 1) * T)
                prod = pair.tile([P, 2, T], F32, name="prod")
                for e in range(2):
                    v_ps = bank()
                    for a in range(CB):
                        nc.tensor.matmul(
                            v_ps[:], lhsT=ev_sb[:, a, rows_of(h, e)], rhs=av[:, a, :], start=(a == 0), stop=(a == CB - 1)
                        )
                    nc.vector.scalar_tensor_tensor(
                        out=prod[:, e, :], in0=v_ps[:], scalar=0.0, in1=xs[:, 2 * h + e, tok], op0=ALU.max, op1=ALU.mult
                    )
                rstd = column_rstd(squares)
                nc.vector.tensor_tensor(
                    out=gated[:, 2 * h : 2 * h + 2, tok], in0=prod[:], in1=rstd[:].unsqueeze(1).to_broadcast([P, 2, T]), op=ALU.mult
                )

            def parts_of(b):
                return HALVES if b == B - 1 else (slice(0, T),)

            def project(b):
                tok = slice(b * T, (b + 1) * T)
                last = b == B - 1
                w_ps = [bank() for a in range(CB)]
                for blocks in (range(0, KB - 2), range(KB - 2, KB)):
                    for a in range(CB):
                        for k in blocks:
                            nc.tensor.matmul(
                                w_ps[a][:],
                                lhsT=dec_c[:, k, a * P : (a + 1) * P],
                                rhs=gated[:, k, tok],
                                start=(k == 0),
                                stop=(k == KB - 1),
                            )
                y = back.tile([P, CB, T], F32, name="y")
                squares_w = []
                for part in parts_of(b):
                    sq = ring.tile([P, CB, part.stop - part.start], BF16, name="sq")
                    for a in range(CB):
                        nc.scalar.activation(out=sq[:, a, :], in_=w_ps[a][:, part], func=ACT.Square)
                    squares_w.append(sq)
                squares = []
                for part, sq_w in zip(parts_of(b), squares_w):
                    rstd = column_rstd(sq_w if last else add_blocks(sq_w), any_bank=last)
                    sq = ring.tile([P, CB, part.stop - part.start], BF16, name="sq")
                    for a in range(CB):
                        nc.vector.tensor_tensor(out=y[:, a, part], in0=w_ps[a][:, part], in1=rstd[:], op=ALU.mult)
                        nc.scalar.activation(out=sq[:, a, :], in_=y[:, a, part], func=ACT.Square, bias=l_c[:, a : a + 1])
                    squares.append(sq)
                return y, squares

            def finish(b, y, squares):
                last = b == B - 1
                res = back.tile([P, CB, T], F32, name="res")
                for part, sq in zip(parts_of(b), squares):
                    rstd = column_rstd(sq if last else add_blocks(sq), any_bank=last)
                    for a in range(CB):
                        nc.vector.scalar_tensor_tensor(
                            out=res[:, a, part], in0=y[:, a, part], scalar=l_c[:, a : a + 1], in1=rstd[:], op0=ALU.add, op1=ALU.mult
                        )
                        nc.sync.dma_start(out[a * P : (a + 1) * P, b * T + part.start : b * T + part.stop], res[:, a, part])

            heads = [(b, h) for b in range(B) for h in range(NH)]
            count = len(heads)
            rotate(*heads[0])
            rotate(*heads[1])
            a_t_of = {0: scores(*heads[0])}
            made_of = {}
            normed_of = {}
            for i in range(count + 3):
                if i + 2 < count:
                    rotate(*heads[i + 2])
                if i + 1 < count:
                    a_t_of[i + 1] = scores(*heads[i + 1])
                if i < count:
                    made_of[i] = values(heads[i][0], a_t_of[i])
                if 0 <= i - 1 < count:
                    gate(*heads[i - 1], *made_of[i - 1])
                if 0 <= i - 2 < count and heads[i - 2][1] == NH - 1:
                    normed_of[i - 2] = project(heads[i - 2][0])
                if 0 <= i - 3 < count and heads[i - 3][1] == NH - 1:
                    finish(heads[i - 3][0], *normed_of[i - 3])
